import numpy as np
import ml_dtypes


def mxq(x, axis, fmt="e4m3"):
    dtype, down = {"e4m3": (ml_dtypes.float8_e4m3fn, 7), "e5m2": (ml_dtypes.float8_e5m2, 14)}[fmt]
    v = np.moveaxis(np.asarray(x, np.float32).astype(ml_dtypes.bfloat16).astype(np.float64), axis, -1)
    blocks = v.reshape(v.shape[:-1] + (-1, 32))
    amax = np.abs(blocks).max(-1, keepdims=True)
    byte = np.maximum(np.where(amax > 0, np.frexp(amax)[1] - 1 + 127, 0) - down, 1)
    scale = np.exp2(byte - 127.0)
    codes = (blocks / scale).astype(np.float32).astype(dtype).astype(np.float64)
    return np.moveaxis((codes * scale).reshape(v.shape), -1, axis)


WIDE = False


def mx_kscale(k):
    if not WIDE:
        return np.ones(k)
    levels = np.array([10, -10, 5, -5, 0])
    a = np.random.permutation(np.resize(levels, k // 512 * 4)).reshape(k // 512, 4)
    idx = np.arange(k)
    return np.exp2(a[idx // 512, idx % 128 // 32])


BF16 = ml_dtypes.bfloat16


def bf(x):
    return np.asarray(x, np.float32).astype(BF16)


def f64(x):
    return np.asarray(x).astype(np.float64)


B, I, J, K, D = 128, 128, 512, 2, 64


def squash(x, axis=-1):
    norm = np.sqrt(np.sum(x * x, axis=axis, keepdims=True))
    scale = norm ** 2 / (1.0 + norm ** 2) / (norm + 1e-8)
    return scale * x


def setup_inputs():
    s = mx_kscale(J)
    c = 2.0 / np.sqrt(J * D * (K * K / 4.0 + K / 12.0))
    return {"X": bf(np.random.standard_normal((B, J, D)) * s[None, :, None]),
            "weight": bf(np.random.random((I, J, K, D)) * c / s[None, :, None, None])}


def reference(X, weight):
    xq = mxq(f64(X), 1, "e4m3")
    wq = mxq(f64(weight).sum(axis=2), 1, "e4m3")
    s = xq.transpose(2, 0, 1) @ wq.transpose(2, 1, 0)
    return squash(s.transpose(1, 2, 0), axis=-1)

@@ -1,0 +1,149 @@
+from contextlib import ExitStack
+
+import concourse.bass as bass
+import concourse.mybir as mybir
+import concourse.tile as tile
+
+FLOPS = 2 * 128 * 128 * 512 * 64
+
+BF16 = mybir.dt.bfloat16
+F32 = mybir.dt.float32
+U32 = mybir.dt.uint32
+U8 = mybir.dt.uint8
+FP8X4 = mybir.dt.float8_e4m3fn_x4
+ACT = mybir.ActivationFunctionType
+ALU = mybir.AluOpType
+
+P = 128
+B = 128
+I = 128
+D = 64
+T = 4
+BC = 16
+IC = 8
+IQ = 32
+DK = 16
+
+
+def tile_primary_capsule_kernel(tc, X, weight, out):
+    nc = tc.nc
+    with ExitStack() as ctx:
+        raw = ctx.enter_context(tc.tile_pool(name="raw", bufs=5))
+        grp = ctx.enter_context(tc.tile_pool(name="grp", bufs=5))
+        keep = ctx.enter_context(tc.tile_pool(name="keep", bufs=1))
+        wq = ctx.enter_context(tc.tile_pool(name="wq", bufs=2))
+        wsp = ctx.enter_context(tc.tile_pool(name="wsp", bufs=3))
+        epi = ctx.enter_context(tc.tile_pool(name="epi", bufs=3))
+        sqp = ctx.enter_context(tc.tile_pool(name="sqp", bufs=1))
+        small = ctx.enter_context(tc.tile_pool(name="small", bufs=2))
+        psum = ctx.enter_context(tc.psum_pool(name="psum", bufs=8))
+
+        warm = keep.tile([P, 1], F32)
+        nc.vector.memset(warm[:], 1.0)
+        nc.scalar.activation(out=warm[:], in_=warm[:], func=ACT.Sqrt)
+
+        x_view = X.rearrange("b (p t) d -> p b (t d)", t=T)
+        w_view = weight.rearrange("i (p t) k d -> p i (t k d)", t=T)
+
+        x_codes = keep.tile([P, D * B], U32, align_bytes=64)
+        x_scales = keep.tile([P, D * B], U8, align_bytes=64)
+
+        gx = []
+        for k in range(D // DK):
+            gxk = grp.tile([P, DK, B, T], BF16, tag="g", name="gx%d" % k, align_bytes=64)
+            gx.append(gxk)
+        for c in range(B // BC):
+            xr = raw.tile([P, BC, T, D], BF16, tag="raw", name="xr")
+            nc.sync.dma_start(
+                out=xr[:].rearrange("p b t d -> p b (t d)"),
+                in_=x_view[:, c * BC:(c + 1) * BC, :],
+            )
+            for k in range(D // DK):
+                src = xr[:, :, :, k * DK:(k + 1) * DK].rearrange("p b t d -> p d b t")
+                dst = gx[k][:, :, c * BC:(c + 1) * BC, :]
+                if k < 2:
+                    nc.vector.tensor_copy(out=dst, in_=src)
+                else:
+                    nc.scalar.copy(out=dst, in_=src)
+        for k in range(D // DK):
+            flat = gx[k][:].rearrange("p d b t -> p (d b t)")
+            for h in range(2):
+                w0 = (k * 2 + h) * 1024
+                nc.vector.quantize_mx(
+                    out=x_codes[:, w0:w0 + 1024].bitcast(FP8X4),
+                    scales=x_scales[:, w0:w0 + 1024],
+                    in_=flat[:, h * 4096:(h + 1) * 4096],
+                )
+
+        for q in range(I // IQ):
+            gw = grp.tile([P, D, IQ, T], BF16, tag="g", name="gw", align_bytes=64)
+            for cc in range(IQ // IC):
+                i0 = q * IQ + cc * IC
+                wr = raw.tile([P, IC * T, 2, D], BF16, tag="raw", name="wr")
+                nc.sync.dma_start(
+                    out=wr[:].rearrange("p (i t) k d -> p i (t k d)", t=T),
+                    in_=w_view[:, i0:i0 + IC, :],
+                )
+                ws = wsp.tile([P, IC, T, D], BF16, name="ws")
+                nc.vector.tensor_tensor(
+                    out=ws[:].rearrange("p i t d -> p (i t) d"),
+                    in0=wr[:, :, 0, :],
+                    in1=wr[:, :, 1, :],
+                    op=ALU.add,
+                )
+                nc.vector.tensor_copy(
+                    out=gw[:, 0:DK, cc * IC:(cc + 1) * IC, :],
+                    in_=ws[:, :, :, 0:DK].rearrange("p i t d -> p d i t"),
+                )
+                nc.scalar.copy(
+                    out=gw[:, DK:D, cc * IC:(cc + 1) * IC, :],
+                    in_=ws[:, :, :, DK:D].rearrange("p i t d -> p d i t"),
+                )
+            w_codes = wq.tile([P, D * IQ], U32, align_bytes=64)
+            w_scales = wq.tile([P, D * IQ], U8, align_bytes=64)
+            gflat = gw[:].rearrange("p d i t -> p (d i t)")
+            for h in range(2):
+                nc.vector.quantize_mx(
+                    out=w_codes[:, h * 1024:(h + 1) * 1024].bitcast(FP8X4),
+                    scales=w_scales[:, h * 1024:(h + 1) * 1024],
+                    in_=gflat[:, h * 4096:(h + 1) * 4096],
+                )
+
+            s_sb = epi.tile([P, IQ, D], F32, name="s_sb")
+            sq = sqp.tile([P, IQ, D], F32, name="sq")
+            for m in range(D // 4):
+                bank = psum.tile([P, 512], F32, name="bank")
+                for r in range(4):
+                    d = 4 * m + r
+                    nc.tensor.matmul_mx(
+                        out=bank[:, r * 128:(r + 1) * 128],
+                        lhsT=x_codes[:, d * B:(d + 1) * B].bitcast(FP8X4),
+                        lhsT_scale=x_scales[:, d * B:(d + 1) * B],
+                        rhs=w_codes[:, m * 128:(m + 1) * 128].bitcast(FP8X4),
+                        rhs_scale=w_scales[:, m * 128:(m + 1) * 128],
+                        start=True,
+                        stop=True,
+                    )
+                diag = bank[:].rearrange("p (a c) -> p a c", c=IQ)[:, 0:16:5, :]
+                diag = diag.rearrange("p r i -> p i r")
+                nc.scalar.copy(out=s_sb[:, :, 4 * m:4 * m + 4], in_=diag)
+                nc.scalar.activation(out=sq[:, :, 4 * m:4 * m + 4], in_=diag, func=ACT.Square)
+
+            n2 = small.tile([P, IQ], F32, name="n2")
+            nc.vector.tensor_reduce(out=n2[:], in_=sq[:], axis=mybir.AxisListType.X, op=ALU.add)
+            ab = small.tile([P, 2 * IQ], F32, name="ab")
+            nc.scalar.activation(out=ab[:, IQ:2 * IQ], in_=n2[:], func=ACT.Sqrt)
+            nc.vector.tensor_scalar_add(out=ab[:, 0:IQ], in0=n2[:], scalar1=1.0)
+            nc.vector.tensor_scalar_add(out=ab[:, IQ:2 * IQ], in0=ab[:, IQ:2 * IQ], scalar1=1e-8)
+            rab = small.tile([P, 2 * IQ], F32, name="rab")
+            nc.vector.reciprocal(out=rab[:], in_=ab[:])
+            f = small.tile([P, IQ], F32, name="f")
+            nc.vector.tensor_tensor(out=f[:], in0=n2[:], in1=rab[:, 0:IQ], op=ALU.mult)
+            nc.vector.tensor_tensor(out=f[:], in0=f[:], in1=rab[:, IQ:2 * IQ], op=ALU.mult)
+            nc.vector.tensor_tensor(
+                out=s_sb[:],
+                in0=s_sb[:],
+                in1=f[:].unsqueeze(2).to_broadcast([P, IQ, D]),
+                op=ALU.mult,
+            )
+            nc.gpsimd.dma_start(out=out[:, q * IQ:(q + 1) * IQ, :], in_=s_sb[:])

@@ -19,8 +19,8 @@ B = 128
 I = 128
 D = 64
 T = 4
-BC = 16
-IC = 8
+BC = 32
+IC = 16
 IQ = 32
 DK = 16
 
@@ -28,12 +28,12 @@ DK = 16
 def tile_primary_capsule_kernel(tc, X, weight, out):
     nc = tc.nc
     with ExitStack() as ctx:
-        raw = ctx.enter_context(tc.tile_pool(name="raw", bufs=5))
+        raw = ctx.enter_context(tc.tile_pool(name="raw", bufs=3))
         grp = ctx.enter_context(tc.tile_pool(name="grp", bufs=5))
         keep = ctx.enter_context(tc.tile_pool(name="keep", bufs=1))
         wq = ctx.enter_context(tc.tile_pool(name="wq", bufs=2))
-        wsp = ctx.enter_context(tc.tile_pool(name="wsp", bufs=3))
-        epi = ctx.enter_context(tc.tile_pool(name="epi", bufs=3))
+        wsp = ctx.enter_context(tc.tile_pool(name="wsp", bufs=2))
+        epi = ctx.enter_context(tc.tile_pool(name="epi", bufs=2))
         sqp = ctx.enter_context(tc.tile_pool(name="sqp", bufs=1))
         small = ctx.enter_context(tc.tile_pool(name="small", bufs=2))
         psum = ctx.enter_context(tc.psum_pool(name="psum", bufs=8))
@@ -59,12 +59,19 @@ def tile_primary_capsule_kernel(tc, X, weight, out):
                 in_=x_view[:, c * BC:(c + 1) * BC, :],
             )
             for k in range(D // DK):
-                src = xr[:, :, :, k * DK:(k + 1) * DK].rearrange("p b t d -> p d b t")
+                src = xr[:, :, :, k * DK:(k + 1) * DK]
                 dst = gx[k][:, :, c * BC:(c + 1) * BC, :]
                 if k < 2:
-                    nc.vector.tensor_copy(out=dst, in_=src)
+                    nc.vector.tensor_copy(
+                        out=dst.rearrange("p (g e) b t -> p g b t e", e=4),
+                        in_=src.rearrange("p b t (g e) -> p g b t e", e=4),
+                    )
                 else:
-                    nc.scalar.copy(out=dst, in_=src)
+                    for g in range(DK // 4):
+                        nc.scalar.copy(
+                            out=dst[:, 4 * g:4 * g + 4, :, :].rearrange("p e b t -> p b t e"),
+                            in_=src[:, :, :, 4 * g:4 * g + 4],
+                        )
         for k in range(D // DK):
             flat = gx[k][:].rearrange("p d b t -> p (d b t)")
             for h in range(2):
@@ -92,13 +99,14 @@ def tile_primary_capsule_kernel(tc, X, weight, out):
                     op=ALU.add,
                 )
                 nc.vector.tensor_copy(
-                    out=gw[:, 0:DK, cc * IC:(cc + 1) * IC, :],
-                    in_=ws[:, :, :, 0:DK].rearrange("p i t d -> p d i t"),
+                    out=gw[:, 0:DK, cc * IC:(cc + 1) * IC, :].rearrange("p (g e) i t -> p g i t e", e=4),
+                    in_=ws[:, :, :, 0:DK].rearrange("p i t (g e) -> p g i t e", e=4),
                 )
-                nc.scalar.copy(
-                    out=gw[:, DK:D, cc * IC:(cc + 1) * IC, :],
-                    in_=ws[:, :, :, DK:D].rearrange("p i t d -> p d i t"),
-                )
+                for g in range(DK // 4, D // 4):
+                    nc.scalar.copy(
+                        out=gw[:, 4 * g:4 * g + 4, cc * IC:(cc + 1) * IC, :].rearrange("p e i t -> p i t e"),
+                        in_=ws[:, :, :, 4 * g:4 * g + 4],
+                    )
             w_codes = wq.tile([P, D * IQ], U32, align_bytes=64)
             w_scales = wq.tile([P, D * IQ], U8, align_bytes=64)
             gflat = gw[:].rearrange("p d i t -> p (d i t)")

@@ -1,8 +1,6 @@
 from contextlib import ExitStack
 
-import concourse.bass as bass
 import concourse.mybir as mybir
-import concourse.tile as tile
 
 FLOPS = 2 * 128 * 128 * 512 * 64
 
@@ -13,6 +11,7 @@ U8 = mybir.dt.uint8
 FP8X4 = mybir.dt.float8_e4m3fn_x4
 ACT = mybir.ActivationFunctionType
 ALU = mybir.AluOpType
+AX = mybir.AxisListType
 
 P = 128
 B = 128
@@ -23,19 +22,25 @@ BC = 32
 IC = 16
 IQ = 32
 DK = 16
+NQ = I // IQ
+KIB = 1024
+PIN = True
+XV = 8
+WV = 6
 
 
 def tile_primary_capsule_kernel(tc, X, weight, out):
     nc = tc.nc
     with ExitStack() as ctx:
+        if PIN:
+            ctx.enter_context(tc.manual_schedule())
         raw = ctx.enter_context(tc.tile_pool(name="raw", bufs=3))
-        grp = ctx.enter_context(tc.tile_pool(name="grp", bufs=5))
         keep = ctx.enter_context(tc.tile_pool(name="keep", bufs=1))
+        gwp = ctx.enter_context(tc.tile_pool(name="gwp", bufs=2))
         wq = ctx.enter_context(tc.tile_pool(name="wq", bufs=2))
         wsp = ctx.enter_context(tc.tile_pool(name="wsp", bufs=2))
-        epi = ctx.enter_context(tc.tile_pool(name="epi", bufs=2))
-        sqp = ctx.enter_context(tc.tile_pool(name="sqp", bufs=1))
         small = ctx.enter_context(tc.tile_pool(name="small", bufs=2))
+        over = ctx.enter_context(tc.tile_pool(name="over", bufs=1))
         psum = ctx.enter_context(tc.psum_pool(name="psum", bufs=8))
 
         warm = keep.tile([P, 1], F32)
@@ -50,65 +55,74 @@ def tile_primary_capsule_kernel(tc, X, weight, out):
 
         gx = []
         for k in range(D // DK):
-            gxk = grp.tile([P, DK, B, T], BF16, tag="g", name="gx%d" % k, align_bytes=64)
+            gxk = over.tile([P, DK, B, T], BF16, name="gx%d" % k, align_bytes=64, offset=k * 16 * KIB)
             gx.append(gxk)
-        for c in range(B // BC):
+
+        def load_regroup_x(c):
             xr = raw.tile([P, BC, T, D], BF16, tag="raw", name="xr")
             nc.sync.dma_start(
                 out=xr[:].rearrange("p b t d -> p b (t d)"),
                 in_=x_view[:, c * BC:(c + 1) * BC, :],
             )
             for k in range(D // DK):
-                src = xr[:, :, :, k * DK:(k + 1) * DK]
+                g_lo = k * (DK // 4)
+                nv = max(0, min(DK // 4, XV - g_lo))
                 dst = gx[k][:, :, c * BC:(c + 1) * BC, :]
-                if k < 2:
+                src = xr[:, :, :, k * DK:(k + 1) * DK]
+                if nv > 0:
                     nc.vector.tensor_copy(
-                        out=dst.rearrange("p (g e) b t -> p g b t e", e=4),
-                        in_=src.rearrange("p b t (g e) -> p g b t e", e=4),
+                        out=dst[:, 0:4 * nv, :, :].rearrange("p (g e) b t -> p g b t e", e=4),
+                        in_=src[:, :, :, 0:4 * nv].rearrange("p b t (g e) -> p g b t e", e=4),
                     )
-                else:
-                    for g in range(DK // 4):
-                        nc.scalar.copy(
-                            out=dst[:, 4 * g:4 * g + 4, :, :].rearrange("p e b t -> p b t e"),
-                            in_=src[:, :, :, 4 * g:4 * g + 4],
-                        )
-        for k in range(D // DK):
-            flat = gx[k][:].rearrange("p d b t -> p (d b t)")
-            for h in range(2):
-                w0 = (k * 2 + h) * 1024
+                for g in range(nv, DK // 4):
+                    nc.scalar.copy(
+                        out=dst[:, 4 * g:4 * g + 4, :, :].rearrange("p e b t -> p b t e"),
+                        in_=src[:, :, :, 4 * g:4 * g + 4],
+                    )
+
+        def quantise_x(h, d_lo, d_hi):
+            for d in range(d_lo, d_hi):
+                w0 = d * B + h * 64
                 nc.vector.quantize_mx(
-                    out=x_codes[:, w0:w0 + 1024].bitcast(FP8X4),
-                    scales=x_scales[:, w0:w0 + 1024],
-                    in_=flat[:, h * 4096:(h + 1) * 4096],
+                    out=x_codes[:, w0:w0 + 64].bitcast(FP8X4),
+                    scales=x_scales[:, w0:w0 + 64],
+                    in_=gx[d // DK][:, d % DK, h * 64:(h + 1) * 64, :].rearrange("p b t -> p (b t)"),
                 )
 
-        for q in range(I // IQ):
-            gw = grp.tile([P, D, IQ, T], BF16, tag="g", name="gw", align_bytes=64)
-            for cc in range(IQ // IC):
-                i0 = q * IQ + cc * IC
-                wr = raw.tile([P, IC * T, 2, D], BF16, tag="raw", name="wr")
-                nc.sync.dma_start(
-                    out=wr[:].rearrange("p (i t) k d -> p i (t k d)", t=T),
-                    in_=w_view[:, i0:i0 + IC, :],
-                )
-                ws = wsp.tile([P, IC, T, D], BF16, name="ws")
-                nc.vector.tensor_tensor(
-                    out=ws[:].rearrange("p i t d -> p (i t) d"),
-                    in0=wr[:, :, 0, :],
-                    in1=wr[:, :, 1, :],
-                    op=ALU.add,
-                )
+        st = {}
+
+        def load_add_regroup_w(q, cc):
+            if cc == 0:
+                st["gw", q] = gwp.tile([P, D, IQ, T], BF16, name="gw", align_bytes=64)
+            gw = st["gw", q]
+            i0 = q * IQ + cc * IC
+            wr = raw.tile([P, IC * T, 2, D], BF16, tag="raw", name="wr")
+            nc.sync.dma_start(
+                out=wr[:].rearrange("p (i t) k d -> p i (t k d)", t=T),
+                in_=w_view[:, i0:i0 + IC, :],
+            )
+            ws = wsp.tile([P, IC, T, D], BF16, name="ws")
+            nc.vector.tensor_tensor(
+                out=ws[:].rearrange("p i t d -> p (i t) d"),
+                in0=wr[:, :, 0, :],
+                in1=wr[:, :, 1, :],
+                op=ALU.add,
+            )
+            if WV > 0:
                 nc.vector.tensor_copy(
-                    out=gw[:, 0:DK, cc * IC:(cc + 1) * IC, :].rearrange("p (g e) i t -> p g i t e", e=4),
-                    in_=ws[:, :, :, 0:DK].rearrange("p i t (g e) -> p g i t e", e=4),
+                    out=gw[:, 0:4 * WV, cc * IC:(cc + 1) * IC, :].rearrange("p (g e) i t -> p g i t e", e=4),
+                    in_=ws[:, :, :, 0:4 * WV].rearrange("p i t (g e) -> p g i t e", e=4),
                 )
-                for g in range(DK // 4, D // 4):
-                    nc.scalar.copy(
-                        out=gw[:, 4 * g:4 * g + 4, cc * IC:(cc + 1) * IC, :].rearrange("p e i t -> p i t e"),
-                        in_=ws[:, :, :, 4 * g:4 * g + 4],
-                    )
-            w_codes = wq.tile([P, D * IQ], U32, align_bytes=64)
-            w_scales = wq.tile([P, D * IQ], U8, align_bytes=64)
+            for g in range(WV, D // 4):
+                nc.scalar.copy(
+                    out=gw[:, 4 * g:4 * g + 4, cc * IC:(cc + 1) * IC, :].rearrange("p e i t -> p i t e"),
+                    in_=ws[:, :, :, 4 * g:4 * g + 4],
+                )
+
+        def quantise_multiply(q):
+            gw = st["gw", q]
+            w_codes = wq.tile([P, D * IQ], U32, align_bytes=64, name="w_codes")
+            w_scales = wq.tile([P, D * IQ], U8, align_bytes=64, name="w_scales")
             gflat = gw[:].rearrange("p d i t -> p (d i t)")
             for h in range(2):
                 nc.vector.quantize_mx(
@@ -116,9 +130,10 @@ def tile_primary_capsule_kernel(tc, X, weight, out):
                     scales=w_scales[:, h * 1024:(h + 1) * 1024],
                     in_=gflat[:, h * 4096:(h + 1) * 4096],
                 )
-
-            s_sb = epi.tile([P, IQ, D], F32, name="s_sb")
-            sq = sqp.tile([P, IQ, D], F32, name="sq")
+            s_sb = over.tile([P, IQ, D], F32, name="s_sb%d" % q, offset=(q % 3) * 8 * KIB)
+            sq = over.tile([P, IQ, D], F32, name="sq%d" % q, offset=(3 + q % 2) * 8 * KIB)
+            st["s", q] = s_sb
+            st["sq", q] = sq
             for m in range(D // 4):
                 bank = psum.tile([P, 512], F32, name="bank")
                 for r in range(4):
@@ -134,13 +149,23 @@ def tile_primary_capsule_kernel(tc, X, weight, out):
                     )
                 diag = bank[:].rearrange("p (a c) -> p a c", c=IQ)[:, 0:16:5, :]
                 diag = diag.rearrange("p r i -> p i r")
-                nc.scalar.copy(out=s_sb[:, :, 4 * m:4 * m + 4], in_=diag)
                 nc.scalar.activation(out=sq[:, :, 4 * m:4 * m + 4], in_=diag, func=ACT.Square)
+                nc.scalar.copy(out=s_sb[:, :, 4 * m:4 * m + 4], in_=diag)
 
+        def norm(q):
+            sq = st["sq", q]
+            n2p = small.tile([P, 4, IQ], F32, name="n2p")
+            for a in range(4):
+                nc.vector.tensor_reduce(out=n2p[:, a, :], in_=sq[:, :, 16 * a:16 * a + 16], axis=AX.X, op=ALU.add)
             n2 = small.tile([P, IQ], F32, name="n2")
-            nc.vector.tensor_reduce(out=n2[:], in_=sq[:], axis=mybir.AxisListType.X, op=ALU.add)
+            nc.vector.tensor_reduce(out=n2[:], in_=n2p[:].rearrange("p a i -> p i a"), axis=AX.X, op=ALU.add)
             ab = small.tile([P, 2 * IQ], F32, name="ab")
             nc.scalar.activation(out=ab[:, IQ:2 * IQ], in_=n2[:], func=ACT.Sqrt)
+            st["n2", q] = (n2, ab)
+
+        def scale_store(q):
+            n2, ab = st["n2", q]
+            s_sb = st["s", q]
             nc.vector.tensor_scalar_add(out=ab[:, 0:IQ], in0=n2[:], scalar1=1.0)
             nc.vector.tensor_scalar_add(out=ab[:, IQ:2 * IQ], in0=ab[:, IQ:2 * IQ], scalar1=1e-8)
             rab = small.tile([P, 2 * IQ], F32, name="rab")
@@ -148,10 +173,33 @@ def tile_primary_capsule_kernel(tc, X, weight, out):
             f = small.tile([P, IQ], F32, name="f")
             nc.vector.tensor_tensor(out=f[:], in0=n2[:], in1=rab[:, 0:IQ], op=ALU.mult)
             nc.vector.tensor_tensor(out=f[:], in0=f[:], in1=rab[:, IQ:2 * IQ], op=ALU.mult)
-            nc.vector.tensor_tensor(
-                out=s_sb[:],
-                in0=s_sb[:],
-                in1=f[:].unsqueeze(2).to_broadcast([P, IQ, D]),
-                op=ALU.mult,
-            )
-            nc.gpsimd.dma_start(out=out[:, q * IQ:(q + 1) * IQ, :], in_=s_sb[:])
+            for h in range(2):
+                rows = slice(h * 16, (h + 1) * 16)
+                nc.vector.tensor_tensor(
+                    out=s_sb[:, rows, :],
+                    in0=s_sb[:, rows, :],
+                    in1=f[:, rows].unsqueeze(2).to_broadcast([P, 16, D]),
+                    op=ALU.mult,
+                )
+                nc.gpsimd.dma_start(out=out[:, q * IQ + h * 16:q * IQ + (h + 1) * 16, :], in_=s_sb[:, rows, :])
+
+        load_regroup_x(0)
+        load_regroup_x(1)
+        quantise_x(0, 0, D)
+        load_regroup_x(2)
+        load_regroup_x(3)
+        for q in range(NQ + 2):
+            if q < NQ:
+                load_add_regroup_w(q, 0)
+            if q == 0:
+                quantise_x(1, 0, D // 2)
+            if q - 2 >= 0:
+                norm(q - 2)
+            if q < NQ:
+                load_add_regroup_w(q, 1)
+            if q == 0:
+                quantise_x(1, D // 2, D)
+            if 0 <= q - 1 < NQ:
+                quantise_multiply(q - 1)
+            if q - 2 >= 0:
+                scale_store(q - 2)

@@ -25,7 +25,7 @@ DK = 16
 NQ = I // IQ
 KIB = 1024
 PIN = True
-XV = 8
+XV = 10
 WV = 6
 
 
@@ -91,16 +91,20 @@ def tile_primary_capsule_kernel(tc, X, weight, out):
 
         st = {}
 
-        def load_add_regroup_w(q, cc):
-            if cc == 0:
-                st["gw", q] = gwp.tile([P, D, IQ, T], BF16, name="gw", align_bytes=64)
-            gw = st["gw", q]
+        def load_w(q, cc):
             i0 = q * IQ + cc * IC
             wr = raw.tile([P, IC * T, 2, D], BF16, tag="raw", name="wr")
             nc.sync.dma_start(
                 out=wr[:].rearrange("p (i t) k d -> p i (t k d)", t=T),
                 in_=w_view[:, i0:i0 + IC, :],
             )
+            st["wr", q, cc] = wr
+
+        def add_regroup_w(q, cc):
+            if cc == 0:
+                st["gw", q] = gwp.tile([P, D, IQ, T], BF16, name="gw", align_bytes=64)
+            gw = st["gw", q]
+            wr = st["wr", q, cc]
             ws = wsp.tile([P, IC, T, D], BF16, name="ws")
             nc.vector.tensor_tensor(
                 out=ws[:].rearrange("p i t d -> p (i t) d"),
@@ -119,7 +123,7 @@ def tile_primary_capsule_kernel(tc, X, weight, out):
                     in_=ws[:, :, :, 4 * g:4 * g + 4],
                 )
 
-        def quantise_multiply(q):
+        def quantise_w(q):
             gw = st["gw", q]
             w_codes = wq.tile([P, D * IQ], U32, align_bytes=64, name="w_codes")
             w_scales = wq.tile([P, D * IQ], U8, align_bytes=64, name="w_scales")
@@ -134,7 +138,12 @@ def tile_primary_capsule_kernel(tc, X, weight, out):
             sq = over.tile([P, IQ, D], F32, name="sq%d" % q, offset=(3 + q % 2) * 8 * KIB)
             st["s", q] = s_sb
             st["sq", q] = sq
-            for m in range(D // 4):
+            st["codes", q] = (w_codes, w_scales)
+
+        def multiply(q, m_lo, m_hi):
+            w_codes, w_scales = st["codes", q]
+            s_sb, sq = st["s", q], st["sq", q]
+            for m in range(m_lo, m_hi):
                 bank = psum.tile([P, 512], F32, name="bank")
                 for r in range(4):
                     d = 4 * m + r
@@ -152,11 +161,15 @@ def tile_primary_capsule_kernel(tc, X, weight, out):
                 nc.scalar.activation(out=sq[:, :, 4 * m:4 * m + 4], in_=diag, func=ACT.Square)
                 nc.scalar.copy(out=s_sb[:, :, 4 * m:4 * m + 4], in_=diag)
 
-        def norm(q):
+        def reduce_part(q, a):
             sq = st["sq", q]
-            n2p = small.tile([P, 4, IQ], F32, name="n2p")
-            for a in range(4):
-                nc.vector.tensor_reduce(out=n2p[:, a, :], in_=sq[:, :, 16 * a:16 * a + 16], axis=AX.X, op=ALU.add)
+            if a == 0:
+                st["n2p", q] = small.tile([P, 4, IQ], F32, name="n2p")
+            n2p = st["n2p", q]
+            nc.vector.tensor_reduce(out=n2p[:, a, :], in_=sq[:, :, 16 * a:16 * a + 16], axis=AX.X, op=ALU.add)
+
+        def norm(q):
+            n2p = st["n2p", q]
             n2 = small.tile([P, IQ], F32, name="n2")
             nc.vector.tensor_reduce(out=n2[:], in_=n2p[:].rearrange("p a i -> p i a"), axis=AX.X, op=ALU.add)
             ab = small.tile([P, 2 * IQ], F32, name="ab")
@@ -181,25 +194,39 @@ def tile_primary_capsule_kernel(tc, X, weight, out):
                     in1=f[:, rows].unsqueeze(2).to_broadcast([P, 16, D]),
                     op=ALU.mult,
                 )
-                nc.gpsimd.dma_start(out=out[:, q * IQ + h * 16:q * IQ + (h + 1) * 16, :], in_=s_sb[:, rows, :])
+                nc.sync.dma_start(out=out[:, q * IQ + h * 16:q * IQ + (h + 1) * 16, :], in_=s_sb[:, rows, :])
 
         load_regroup_x(0)
         load_regroup_x(1)
         quantise_x(0, 0, D)
         load_regroup_x(2)
         load_regroup_x(3)
-        for q in range(NQ + 2):
-            if q < NQ:
-                load_add_regroup_w(q, 0)
-            if q == 0:
-                quantise_x(1, 0, D // 2)
-            if q - 2 >= 0:
-                norm(q - 2)
-            if q < NQ:
-                load_add_regroup_w(q, 1)
-            if q == 0:
-                quantise_x(1, D // 2, D)
-            if 0 <= q - 1 < NQ:
-                quantise_multiply(q - 1)
-            if q - 2 >= 0:
-                scale_store(q - 2)
+        load_w(0, 0)
+        load_w(0, 1)
+        quantise_x(1, 0, D)
+        NS = 2 * NQ
+        for n in range(NS + 3):
+            r, cc = n // 2, n % 2
+            rp = r - 1
+            if n + 2 < NS:
+                load_w((n + 2) // 2, n % 2)
+            if n < NS:
+                add_regroup_w(r, cc)
+            if cc == 0 and 0 <= rp < NQ:
+                quantise_w(rp)
+                multiply(rp, 0, 8)
+                if rp >= 1:
+                    reduce_part(rp - 1, 2)
+                    reduce_part(rp - 1, 3)
+                    norm(rp - 1)
+            if cc == 1 and 0 <= rp < NQ:
+                multiply(rp, 8, 16)
+                if rp >= 1:
+                    scale_store(rp - 1)
+                reduce_part(rp, 0)
+                reduce_part(rp, 1)
+            if cc == 0 and rp == NQ:
+                reduce_part(NQ - 1, 2)
+                reduce_part(NQ - 1, 3)
+                norm(NQ - 1)
+                scale_store(NQ - 1)

@@ -26,7 +26,7 @@ NQ = I // IQ
 KIB = 1024
 PIN = True
 XV = 10
-WV = 6
+WV = 8
 
 
 def tile_primary_capsule_kernel(tc, X, weight, out):
@@ -90,6 +90,7 @@ def tile_primary_capsule_kernel(tc, X, weight, out):
                 )
 
         st = {}
+        junk = keep.tile([P, D], F32)
 
         def load_w(q, cc):
             i0 = q * IQ + cc * IC
@@ -117,6 +118,10 @@ def tile_primary_capsule_kernel(tc, X, weight, out):
                     out=gw[:, 0:4 * WV, cc * IC:(cc + 1) * IC, :].rearrange("p (g e) i t -> p g i t e", e=4),
                     in_=ws[:, :, :, 0:4 * WV].rearrange("p i t (g e) -> p g i t e", e=4),
                 )
+            st["ws", q, cc] = ws
+
+        def regroup_w_scalar(q, cc):
+            gw, ws = st["gw", q], st["ws", q, cc]
             for g in range(WV, D // 4):
                 nc.scalar.copy(
                     out=gw[:, 4 * g:4 * g + 4, cc * IC:(cc + 1) * IC, :].rearrange("p e i t -> p i t e"),
@@ -135,14 +140,14 @@ def tile_primary_capsule_kernel(tc, X, weight, out):
                     in_=gflat[:, h * 4096:(h + 1) * 4096],
                 )
             s_sb = over.tile([P, IQ, D], F32, name="s_sb%d" % q, offset=(q % 3) * 8 * KIB)
-            sq = over.tile([P, IQ, D], F32, name="sq%d" % q, offset=(3 + q % 2) * 8 * KIB)
             st["s", q] = s_sb
-            st["sq", q] = sq
+            if q == NQ - 1:
+                st["sq", q] = over.tile([P, IQ, D], F32, name="sq", offset=3 * 8 * KIB)
             st["codes", q] = (w_codes, w_scales)
 
         def multiply(q, m_lo, m_hi):
             w_codes, w_scales = st["codes", q]
-            s_sb, sq = st["s", q], st["sq", q]
+            s_sb = st["s", q]
             for m in range(m_lo, m_hi):
                 bank = psum.tile([P, 512], F32, name="bank")
                 for r in range(4):
@@ -158,8 +163,23 @@ def tile_primary_capsule_kernel(tc, X, weight, out):
                     )
                 diag = bank[:].rearrange("p (a c) -> p a c", c=IQ)[:, 0:16:5, :]
                 diag = diag.rearrange("p r i -> p i r")
-                nc.scalar.activation(out=sq[:, :, 4 * m:4 * m + 4], in_=diag, func=ACT.Square)
+                if q == NQ - 1:
+                    nc.scalar.activation(out=st["sq", q][:, :, 4 * m:4 * m + 4], in_=diag, func=ACT.Square)
                 nc.scalar.copy(out=s_sb[:, :, 4 * m:4 * m + 4], in_=diag)
+
+        def square_sum(q, h):
+            if h == 0:
+                st["acc", q] = small.tile([P, IQ], F32, name="n2")
+            n2 = st["acc", q]
+            for i in range(h * 16, (h + 1) * 16):
+                nc.scalar.activation(out=junk[:], in_=st["s", q][:, i, :], func=ACT.Square, accum_out=n2[:, i:i + 1])
+            if h == 1:
+                root(q, n2)
+
+        def root(q, n2):
+            ab = small.tile([P, 2 * IQ], F32, name="ab")
+            nc.scalar.activation(out=ab[:, IQ:2 * IQ], in_=n2[:], func=ACT.Sqrt)
+            st["n2", q] = (n2, ab)
 
         def reduce_part(q, a):
             sq = st["sq", q]
@@ -172,9 +192,7 @@ def tile_primary_capsule_kernel(tc, X, weight, out):
             n2p = st["n2p", q]
             n2 = small.tile([P, IQ], F32, name="n2")
             nc.vector.tensor_reduce(out=n2[:], in_=n2p[:].rearrange("p a i -> p i a"), axis=AX.X, op=ALU.add)
-            ab = small.tile([P, 2 * IQ], F32, name="ab")
-            nc.scalar.activation(out=ab[:, IQ:2 * IQ], in_=n2[:], func=ACT.Sqrt)
-            st["n2", q] = (n2, ab)
+            root(q, n2)
 
         def scale_store(q):
             n2, ab = st["n2", q]
@@ -208,25 +226,33 @@ def tile_primary_capsule_kernel(tc, X, weight, out):
         for n in range(NS + 3):
             r, cc = n // 2, n % 2
             rp = r - 1
+            last = NQ - 1
             if n + 2 < NS:
                 load_w((n + 2) // 2, n % 2)
             if n < NS:
                 add_regroup_w(r, cc)
-            if cc == 0 and 0 <= rp < NQ:
-                quantise_w(rp)
-                multiply(rp, 0, 8)
-                if rp >= 1:
-                    reduce_part(rp - 1, 2)
-                    reduce_part(rp - 1, 3)
-                    norm(rp - 1)
-            if cc == 1 and 0 <= rp < NQ:
-                multiply(rp, 8, 16)
-                if rp >= 1:
+            if cc == 0:
+                if 1 <= rp <= last:
+                    square_sum(rp - 1, 1)
+                if n < NS:
+                    regroup_w_scalar(r, cc)
+                if 0 <= rp <= last:
+                    quantise_w(rp)
+                    multiply(rp, 0, 8)
+                if rp == last:
+                    reduce_part(rp, 0)
+                    reduce_part(rp, 1)
+            else:
+                if 0 <= rp <= last:
+                    multiply(rp, 8, 16)
+                if n < NS:
+                    regroup_w_scalar(r, cc)
+                if 1 <= rp <= last:
                     scale_store(rp - 1)
-                reduce_part(rp, 0)
-                reduce_part(rp, 1)
-            if cc == 0 and rp == NQ:
-                reduce_part(NQ - 1, 2)
-                reduce_part(NQ - 1, 3)
-                norm(NQ - 1)
-                scale_store(NQ - 1)
+                if 0 <= rp < last:
+                    square_sum(rp, 0)
+                if rp == last:
+                    reduce_part(rp, 2)
+                    reduce_part(rp, 3)
+                    norm(rp)
+                    scale_store(rp)

@@ -90,7 +90,6 @@ def tile_primary_capsule_kernel(tc, X, weight, out):
                 )
 
         st = {}
-        junk = keep.tile([P, D], F32)
 
         def load_w(q, cc):
             i0 = q * IQ + cc * IC
@@ -141,8 +140,7 @@ def tile_primary_capsule_kernel(tc, X, weight, out):
                 )
             s_sb = over.tile([P, IQ, D], F32, name="s_sb%d" % q, offset=(q % 3) * 8 * KIB)
             st["s", q] = s_sb
-            if q == NQ - 1:
-                st["sq", q] = over.tile([P, IQ, D], F32, name="sq", offset=3 * 8 * KIB)
+            st["sq", q] = over.tile([P, IQ, D], F32, name="sq%d" % q, offset=(3 + q % 2) * 8 * KIB)
             st["codes", q] = (w_codes, w_scales)
 
         def multiply(q, m_lo, m_hi):
@@ -172,7 +170,9 @@ def tile_primary_capsule_kernel(tc, X, weight, out):
                 st["acc", q] = small.tile([P, IQ], F32, name="n2")
             n2 = st["acc", q]
             for i in range(h * 16, (h + 1) * 16):
-                nc.scalar.activation(out=junk[:], in_=st["s", q][:, i, :], func=ACT.Square, accum_out=n2[:, i:i + 1])
+                nc.scalar.activation(
+                    out=st["sq", q][:, i, :], in_=st["s", q][:, i, :], func=ACT.Square, accum_out=n2[:, i:i + 1]
+                )
             if h == 1:
                 root(q, n2)
 

@@ -74,10 +74,10 @@ def tile_primary_capsule_kernel(tc, X, weight, out):
                         out=dst[:, 0:4 * nv, :, :].rearrange("p (g e) b t -> p g b t e", e=4),
                         in_=src[:, :, :, 0:4 * nv].rearrange("p b t (g e) -> p g b t e", e=4),
                     )
-                for g in range(nv, DK // 4):
+                if nv < DK // 4:
                     nc.scalar.copy(
-                        out=dst[:, 4 * g:4 * g + 4, :, :].rearrange("p e b t -> p b t e"),
-                        in_=src[:, :, :, 4 * g:4 * g + 4],
+                        out=dst[:, 4 * nv:DK, :, :].rearrange("p (g e) b t -> p g b t e", e=4),
+                        in_=src[:, :, :, 4 * nv:DK].rearrange("p b t (g e) -> p g b t e", e=4),
                     )
 
         def quantise_x(h, d_lo, d_hi):
@@ -94,54 +94,57 @@ def tile_primary_capsule_kernel(tc, X, weight, out):
         def load_w(q, cc):
             i0 = q * IQ + cc * IC
             wr = raw.tile([P, IC * T, 2, D], BF16, tag="raw", name="wr")
-            nc.sync.dma_start(
-                out=wr[:].rearrange("p (i t) k d -> p i (t k d)", t=T),
-                in_=w_view[:, i0:i0 + IC, :],
-            )
+            for h in range(2):
+                nc.sync.dma_start(
+                    out=wr[:, h * IC * T // 2:(h + 1) * IC * T // 2, :, :].rearrange("p (i t) k d -> p i (t k d)", t=T),
+                    in_=w_view[:, i0 + h * IC // 2:i0 + (h + 1) * IC // 2, :],
+                )
             st["wr", q, cc] = wr
 
-        def add_regroup_w(q, cc):
-            if cc == 0:
-                st["gw", q] = gwp.tile([P, D, IQ, T], BF16, name="gw", align_bytes=64)
-            gw = st["gw", q]
+        def add_w(q, cc, h):
             wr = st["wr", q, cc]
-            ws = wsp.tile([P, IC, T, D], BF16, name="ws")
+            if h == 0:
+                st["ws", q, cc] = wsp.tile([P, IC, T, D], BF16, name="ws")
+            ws = st["ws", q, cc]
+            rows = slice(h * IC * T // 2, (h + 1) * IC * T // 2)
             nc.vector.tensor_tensor(
-                out=ws[:].rearrange("p i t d -> p (i t) d"),
-                in0=wr[:, :, 0, :],
-                in1=wr[:, :, 1, :],
+                out=ws[:].rearrange("p i t d -> p (i t) d")[:, rows, :],
+                in0=wr[:, rows, 0, :],
+                in1=wr[:, rows, 1, :],
                 op=ALU.add,
             )
-            if WV > 0:
-                nc.vector.tensor_copy(
-                    out=gw[:, 0:4 * WV, cc * IC:(cc + 1) * IC, :].rearrange("p (g e) i t -> p g i t e", e=4),
-                    in_=ws[:, :, :, 0:4 * WV].rearrange("p i t (g e) -> p g i t e", e=4),
-                )
-            st["ws", q, cc] = ws
+
+        def regroup_w_vector(q, cc):
+            if cc == 0:
+                st["gw", q] = gwp.tile([P, D, IQ, T], BF16, name="gw", align_bytes=64)
+            gw, ws = st["gw", q], st["ws", q, cc]
+            nc.vector.tensor_copy(
+                out=gw[:, 0:4 * WV, cc * IC:(cc + 1) * IC, :].rearrange("p (g e) i t -> p g i t e", e=4),
+                in_=ws[:, :, :, 0:4 * WV].rearrange("p i t (g e) -> p g i t e", e=4),
+            )
 
         def regroup_w_scalar(q, cc):
             gw, ws = st["gw", q], st["ws", q, cc]
-            for g in range(WV, D // 4):
+            for g in range(WV, D // 4, 4):
                 nc.scalar.copy(
-                    out=gw[:, 4 * g:4 * g + 4, cc * IC:(cc + 1) * IC, :].rearrange("p e i t -> p i t e"),
-                    in_=ws[:, :, :, 4 * g:4 * g + 4],
+                    out=gw[:, 4 * g:4 * g + 16, cc * IC:(cc + 1) * IC, :].rearrange("p (g e) i t -> p g i t e", e=4),
+                    in_=ws[:, :, :, 4 * g:4 * g + 16].rearrange("p i t (g e) -> p g i t e", e=4),
                 )
 
-        def quantise_w(q):
-            gw = st["gw", q]
-            w_codes = wq.tile([P, D * IQ], U32, align_bytes=64, name="w_codes")
-            w_scales = wq.tile([P, D * IQ], U8, align_bytes=64, name="w_scales")
-            gflat = gw[:].rearrange("p d i t -> p (d i t)")
-            for h in range(2):
-                nc.vector.quantize_mx(
-                    out=w_codes[:, h * 1024:(h + 1) * 1024].bitcast(FP8X4),
-                    scales=w_scales[:, h * 1024:(h + 1) * 1024],
-                    in_=gflat[:, h * 4096:(h + 1) * 4096],
-                )
-            s_sb = over.tile([P, IQ, D], F32, name="s_sb%d" % q, offset=(q % 3) * 8 * KIB)
-            st["s", q] = s_sb
-            st["sq", q] = over.tile([P, IQ, D], F32, name="sq%d" % q, offset=(3 + q % 2) * 8 * KIB)
-            st["codes", q] = (w_codes, w_scales)
+        def quantise_w(q, h):
+            if h == 0:
+                w_codes = wq.tile([P, D * IQ], U32, align_bytes=64, name="w_codes")
+                w_scales = wq.tile([P, D * IQ], U8, align_bytes=64, name="w_scales")
+                st["codes", q] = (w_codes, w_scales)
+                st["s", q] = over.tile([P, IQ, D], F32, name="s_sb%d" % q, offset=(q % 3) * 8 * KIB)
+                st["sq", q] = over.tile([P, IQ, D], F32, name="sq%d" % q, offset=(3 + q % 2) * 8 * KIB)
+            w_codes, w_scales = st["codes", q]
+            gflat = st["gw", q][:].rearrange("p d i t -> p (d i t)")
+            nc.vector.quantize_mx(
+                out=w_codes[:, h * 1024:(h + 1) * 1024].bitcast(FP8X4),
+                scales=w_scales[:, h * 1024:(h + 1) * 1024],
+                in_=gflat[:, h * 4096:(h + 1) * 4096],
+            )
 
         def multiply(q, m_lo, m_hi):
             w_codes, w_scales = st["codes", q]
@@ -163,23 +166,25 @@ def tile_primary_capsule_kernel(tc, X, weight, out):
                 diag = diag.rearrange("p r i -> p i r")
                 if q == NQ - 1:
                     nc.scalar.activation(out=st["sq", q][:, :, 4 * m:4 * m + 4], in_=diag, func=ACT.Square)
-                nc.scalar.copy(out=s_sb[:, :, 4 * m:4 * m + 4], in_=diag)
+                    nc.vector.tensor_copy(out=s_sb[:, :, 4 * m:4 * m + 4], in_=diag)
+                else:
+                    nc.scalar.copy(out=s_sb[:, :, 4 * m:4 * m + 4], in_=diag)
 
-        def square_sum(q, h):
-            if h == 0:
+        def square_sum(q, i_lo, i_hi):
+            if i_lo == 0:
                 st["acc", q] = small.tile([P, IQ], F32, name="n2")
             n2 = st["acc", q]
-            for i in range(h * 16, (h + 1) * 16):
+            for i in range(i_lo, i_hi):
                 nc.scalar.activation(
                     out=st["sq", q][:, i, :], in_=st["s", q][:, i, :], func=ACT.Square, accum_out=n2[:, i:i + 1]
                 )
-            if h == 1:
+            if i_hi == IQ:
                 root(q, n2)
 
         def root(q, n2):
-            ab = small.tile([P, 2 * IQ], F32, name="ab")
-            nc.scalar.activation(out=ab[:, IQ:2 * IQ], in_=n2[:], func=ACT.Sqrt)
-            st["n2", q] = (n2, ab)
+            rt = small.tile([P, IQ], F32, name="rt")
+            nc.scalar.activation(out=rt[:], in_=n2[:], func=ACT.Sqrt)
+            st["n2", q] = (n2, rt)
 
         def reduce_part(q, a):
             sq = st["sq", q]
@@ -194,25 +199,33 @@ def tile_primary_capsule_kernel(tc, X, weight, out):
             nc.vector.tensor_reduce(out=n2[:], in_=n2p[:].rearrange("p a i -> p i a"), axis=AX.X, op=ALU.add)
             root(q, n2)
 
-        def scale_store(q):
-            n2, ab = st["n2", q]
-            s_sb = st["s", q]
-            nc.vector.tensor_scalar_add(out=ab[:, 0:IQ], in0=n2[:], scalar1=1.0)
-            nc.vector.tensor_scalar_add(out=ab[:, IQ:2 * IQ], in0=ab[:, IQ:2 * IQ], scalar1=1e-8)
-            rab = small.tile([P, 2 * IQ], F32, name="rab")
-            nc.vector.reciprocal(out=rab[:], in_=ab[:])
-            f = small.tile([P, IQ], F32, name="f")
-            nc.vector.tensor_tensor(out=f[:], in0=n2[:], in1=rab[:, 0:IQ], op=ALU.mult)
-            nc.vector.tensor_tensor(out=f[:], in0=f[:], in1=rab[:, IQ:2 * IQ], op=ALU.mult)
-            for h in range(2):
-                rows = slice(h * 16, (h + 1) * 16)
-                nc.vector.tensor_tensor(
-                    out=s_sb[:, rows, :],
-                    in0=s_sb[:, rows, :],
-                    in1=f[:, rows].unsqueeze(2).to_broadcast([P, 16, D]),
-                    op=ALU.mult,
+        def factor(q, step):
+            n2, rt = st["n2", q]
+            if step == 0:
+                st["den", q] = small.tile([P, IQ], F32, name="den")
+                nc.vector.tensor_scalar_add(out=st["den", q][:], in0=n2[:], scalar1=1.0)
+            if step == 1:
+                st["den2", q] = small.tile([P, IQ], F32, name="den2")
+                nc.vector.scalar_tensor_tensor(
+                    out=st["den2", q][:], in0=rt[:], scalar=1e-8, in1=st["den", q][:], op0=ALU.add, op1=ALU.mult
                 )
-                nc.sync.dma_start(out=out[:, q * IQ + h * 16:q * IQ + (h + 1) * 16, :], in_=s_sb[:, rows, :])
+            if step == 2:
+                st["rec", q] = small.tile([P, IQ], F32, name="rec")
+                nc.vector.reciprocal(out=st["rec", q][:], in_=st["den2", q][:])
+            if step == 3:
+                st["f", q] = small.tile([P, IQ], F32, name="f")
+                nc.vector.tensor_tensor(out=st["f", q][:], in0=n2[:], in1=st["rec", q][:], op=ALU.mult)
+
+        def scale_store(q, h):
+            s_sb = st["s", q]
+            rows = slice(h * 16, (h + 1) * 16)
+            nc.vector.tensor_tensor(
+                out=s_sb[:, rows, :],
+                in0=s_sb[:, rows, :],
+                in1=st["f", q][:, rows].unsqueeze(2).to_broadcast([P, 16, D]),
+                op=ALU.mult,
+            )
+            nc.sync.dma_start(out=out[:, q * IQ + h * 16:q * IQ + (h + 1) * 16, :], in_=s_sb[:, rows, :])
 
         load_regroup_x(0)
         load_regroup_x(1)
@@ -221,38 +234,69 @@ def tile_primary_capsule_kernel(tc, X, weight, out):
         load_regroup_x(3)
         load_w(0, 0)
         load_w(0, 1)
-        quantise_x(1, 0, D)
         NS = 2 * NQ
-        for n in range(NS + 3):
+        last = NQ - 1
+        for n in range(NS):
             r, cc = n // 2, n % 2
             rp = r - 1
-            last = NQ - 1
             if n + 2 < NS:
                 load_w((n + 2) // 2, n % 2)
-            if n < NS:
-                add_regroup_w(r, cc)
             if cc == 0:
-                if 1 <= rp <= last:
-                    square_sum(rp - 1, 1)
-                if n < NS:
-                    regroup_w_scalar(r, cc)
-                if 0 <= rp <= last:
-                    quantise_w(rp)
+                add_w(r, cc, 0)
+                add_w(r, cc, 1)
+                if n == 0:
+                    quantise_x(1, 0, D // 2)
+                if rp >= 1:
+                    square_sum(rp - 1, 16, 32)
+                if rp >= 0:
+                    quantise_w(rp, 0)
+                regroup_w_vector(r, cc)
+                regroup_w_scalar(r, cc)
+                if rp >= 0:
+                    quantise_w(rp, 1)
                     multiply(rp, 0, 8)
-                if rp == last:
-                    reduce_part(rp, 0)
-                    reduce_part(rp, 1)
+                if rp >= 1:
+                    factor(rp - 1, 0)
             else:
-                if 0 <= rp <= last:
+                if rp >= 0:
                     multiply(rp, 8, 16)
-                if n < NS:
-                    regroup_w_scalar(r, cc)
-                if 1 <= rp <= last:
-                    scale_store(rp - 1)
-                if 0 <= rp < last:
-                    square_sum(rp, 0)
-                if rp == last:
-                    reduce_part(rp, 2)
-                    reduce_part(rp, 3)
-                    norm(rp)
-                    scale_store(rp)
+                if rp >= 1:
+                    factor(rp - 1, 1)
+                add_w(r, cc, 0)
+                if rp >= 1:
+                    factor(rp - 1, 2)
+                add_w(r, cc, 1)
+                if n == 1:
+                    quantise_x(1, D // 2, D)
+                if rp >= 1:
+                    factor(rp - 1, 3)
+                regroup_w_vector(r, cc)
+                regroup_w_scalar(r, cc)
+                if rp >= 1:
+                    scale_store(rp - 1, 0)
+                    scale_store(rp - 1, 1)
+                if rp >= 0:
+                    square_sum(rp, 0, 16)
+        quantise_w(last, 0)
+        quantise_w(last, 1)
+        multiply(last, 0, 4)
+        square_sum(last - 1, 16, 24)
+        multiply(last, 4, 8)
+        square_sum(last - 1, 24, 32)
+        reduce_part(last, 0)
+        factor(last - 1, 0)
+        factor(last - 1, 1)
+        multiply(last, 8, 12)
+        reduce_part(last, 1)
+        factor(last - 1, 2)
+        reduce_part(last, 2)
+        factor(last - 1, 3)
+        scale_store(last - 1, 0)
+        scale_store(last - 1, 1)
+        multiply(last, 12, 16)
+        reduce_part(last, 3)
+        norm(last)
+        for step in range(4):
+            factor(last, step)
+        scale_store(last, 0)
+        scale_store(last, 1)

@@ -27,6 +27,7 @@ KIB = 1024
 PIN = True
 XV = 10
 WV = 8
+WV0 = 0
 
 
 def tile_primary_capsule_kernel(tc, X, weight, out):
@@ -118,14 +119,16 @@ def tile_primary_capsule_kernel(tc, X, weight, out):
             if cc == 0:
                 st["gw", q] = gwp.tile([P, D, IQ, T], BF16, name="gw", align_bytes=64)
             gw, ws = st["gw", q], st["ws", q, cc]
-            nc.vector.tensor_copy(
-                out=gw[:, 0:4 * WV, cc * IC:(cc + 1) * IC, :].rearrange("p (g e) i t -> p g i t e", e=4),
-                in_=ws[:, :, :, 0:4 * WV].rearrange("p i t (g e) -> p g i t e", e=4),
-            )
+            wv = WV0 if q == 0 else WV
+            if wv > 0:
+                nc.vector.tensor_copy(
+                    out=gw[:, 0:4 * wv, cc * IC:(cc + 1) * IC, :].rearrange("p (g e) i t -> p g i t e", e=4),
+                    in_=ws[:, :, :, 0:4 * wv].rearrange("p i t (g e) -> p g i t e", e=4),
+                )
 
         def regroup_w_scalar(q, cc):
             gw, ws = st["gw", q], st["ws", q, cc]
-            for g in range(WV, D // 4, 4):
+            for g in range(WV0 if q == 0 else WV, D // 4, 4):
                 nc.scalar.copy(
                     out=gw[:, 4 * g:4 * g + 16, cc * IC:(cc + 1) * IC, :].rearrange("p (g e) i t -> p g i t e", e=4),
                     in_=ws[:, :, :, 4 * g:4 * g + 16].rearrange("p i t (g e) -> p g i t e", e=4),
@@ -193,10 +196,14 @@ def tile_primary_capsule_kernel(tc, X, weight, out):
             n2p = st["n2p", q]
             nc.vector.tensor_reduce(out=n2p[:, a, :], in_=sq[:, :, 16 * a:16 * a + 16], axis=AX.X, op=ALU.add)
 
+        def sum_so_far(q):
+            nc.vector.tensor_reduce(
+                out=st["sq", q][:, :, 47], in_=st["n2p", q][:, 0:3, :].rearrange("p a i -> p i a"), axis=AX.X, op=ALU.add
+            )
+
         def norm(q):
-            n2p = st["n2p", q]
             n2 = small.tile([P, IQ], F32, name="n2")
-            nc.vector.tensor_reduce(out=n2[:], in_=n2p[:].rearrange("p a i -> p i a"), axis=AX.X, op=ALU.add)
+            nc.vector.tensor_reduce(out=n2[:], in_=st["sq", q][:, :, 47:D], axis=AX.X, op=ALU.add)
             root(q, n2)
 
         def factor(q, step):
@@ -216,16 +223,16 @@ def tile_primary_capsule_kernel(tc, X, weight, out):
                 st["f", q] = small.tile([P, IQ], F32, name="f")
                 nc.vector.tensor_tensor(out=st["f", q][:], in0=n2[:], in1=st["rec", q][:], op=ALU.mult)
 
-        def scale_store(q, h):
+        def scale_store(q, h, n_rows=16):
             s_sb = st["s", q]
-            rows = slice(h * 16, (h + 1) * 16)
+            rows = slice(h * n_rows, (h + 1) * n_rows)
             nc.vector.tensor_tensor(
                 out=s_sb[:, rows, :],
                 in0=s_sb[:, rows, :],
-                in1=st["f", q][:, rows].unsqueeze(2).to_broadcast([P, 16, D]),
+                in1=st["f", q][:, rows].unsqueeze(2).to_broadcast([P, n_rows, D]),
                 op=ALU.mult,
             )
-            nc.sync.dma_start(out=out[:, q * IQ + h * 16:q * IQ + (h + 1) * 16, :], in_=s_sb[:, rows, :])
+            nc.sync.dma_start(out=out[:, q * IQ + h * n_rows:q * IQ + (h + 1) * n_rows, :], in_=s_sb[:, rows, :])
 
         load_regroup_x(0)
         load_regroup_x(1)
@@ -291,12 +298,12 @@ def tile_primary_capsule_kernel(tc, X, weight, out):
         factor(last - 1, 2)
         reduce_part(last, 2)
         factor(last - 1, 3)
+        sum_so_far(last)
         scale_store(last - 1, 0)
         scale_store(last - 1, 1)
         multiply(last, 12, 16)
-        reduce_part(last, 3)
         norm(last)
         for step in range(4):
             factor(last, step)
-        scale_store(last, 0)
-        scale_store(last, 1)
+        for h in range(4):
+            scale_store(last, h, 8)

@@ -59,17 +59,26 @@ def tile_primary_capsule_kernel(tc, X, weight, out):
             gxk = over.tile([P, DK, B, T], BF16, name="gx%d" % k, align_bytes=64, offset=k * 16 * KIB)
             gx.append(gxk)
 
-        def load_regroup_x(c):
+        def load_regroup_x(c, pieces):
             xr = raw.tile([P, BC, T, D], BF16, tag="raw", name="xr")
-            nc.sync.dma_start(
-                out=xr[:].rearrange("p b t d -> p b (t d)"),
-                in_=x_view[:, c * BC:(c + 1) * BC, :],
-            )
+            b0 = 0
+            for rows in pieces:
+                nc.sync.dma_start(
+                    out=xr[:, b0:b0 + rows, :, :].rearrange("p b t d -> p b (t d)"),
+                    in_=x_view[:, c * BC + b0:c * BC + b0 + rows, :],
+                )
+                b0 += rows
+            b0 = 0
+            for rows in pieces:
+                regroup_x(xr, c, b0, rows)
+                b0 += rows
+
+        def regroup_x(xr, c, b0, rows):
             for k in range(D // DK):
                 g_lo = k * (DK // 4)
                 nv = max(0, min(DK // 4, XV - g_lo))
-                dst = gx[k][:, :, c * BC:(c + 1) * BC, :]
-                src = xr[:, :, :, k * DK:(k + 1) * DK]
+                dst = gx[k][:, :, c * BC + b0:c * BC + b0 + rows, :]
+                src = xr[:, b0:b0 + rows, :, k * DK:(k + 1) * DK]
                 if nv > 0:
                     nc.vector.tensor_copy(
                         out=dst[:, 0:4 * nv, :, :].rearrange("p (g e) b t -> p g b t e", e=4),
@@ -134,7 +143,7 @@ def tile_primary_capsule_kernel(tc, X, weight, out):
                     in_=ws[:, :, :, 4 * g:4 * g + 16].rearrange("p i t (g e) -> p g i t e", e=4),
                 )
 
-        def quantise_w(q, h):
+        def quantise_w(q, h, parts=2):
             if h == 0:
                 w_codes = wq.tile([P, D * IQ], U32, align_bytes=64, name="w_codes")
                 w_scales = wq.tile([P, D * IQ], U8, align_bytes=64, name="w_scales")
@@ -143,10 +152,11 @@ def tile_primary_capsule_kernel(tc, X, weight, out):
                 st["sq", q] = over.tile([P, IQ, D], F32, name="sq%d" % q, offset=(3 + q % 2) * 8 * KIB)
             w_codes, w_scales = st["codes", q]
             gflat = st["gw", q][:].rearrange("p d i t -> p (d i t)")
+            words = D * IQ // parts
             nc.vector.quantize_mx(
-                out=w_codes[:, h * 1024:(h + 1) * 1024].bitcast(FP8X4),
-                scales=w_scales[:, h * 1024:(h + 1) * 1024],
-                in_=gflat[:, h * 4096:(h + 1) * 4096],
+                out=w_codes[:, h * words:(h + 1) * words].bitcast(FP8X4),
+                scales=w_scales[:, h * words:(h + 1) * words],
+                in_=gflat[:, h * words * T:(h + 1) * words * T],
             )
 
         def multiply(q, m_lo, m_hi):
@@ -223,22 +233,26 @@ def tile_primary_capsule_kernel(tc, X, weight, out):
                 st["f", q] = small.tile([P, IQ], F32, name="f")
                 nc.vector.tensor_tensor(out=st["f", q][:], in0=n2[:], in1=st["rec", q][:], op=ALU.mult)
 
-        def scale_store(q, h, n_rows=16):
+        def scale_store(q, h, n_rows=16, on_scalar=False):
             s_sb = st["s", q]
             rows = slice(h * n_rows, (h + 1) * n_rows)
-            nc.vector.tensor_tensor(
-                out=s_sb[:, rows, :],
-                in0=s_sb[:, rows, :],
-                in1=st["f", q][:, rows].unsqueeze(2).to_broadcast([P, n_rows, D]),
-                op=ALU.mult,
-            )
+            if on_scalar:
+                for i in range(h * n_rows, (h + 1) * n_rows):
+                    nc.scalar.activation(out=s_sb[:, i, :], in_=s_sb[:, i, :], func=ACT.Copy, scale=st["f", q][:, i:i + 1])
+            else:
+                nc.vector.tensor_tensor(
+                    out=s_sb[:, rows, :],
+                    in0=s_sb[:, rows, :],
+                    in1=st["f", q][:, rows].unsqueeze(2).to_broadcast([P, n_rows, D]),
+                    op=ALU.mult,
+                )
             nc.sync.dma_start(out=out[:, q * IQ + h * n_rows:q * IQ + (h + 1) * n_rows, :], in_=s_sb[:, rows, :])
 
-        load_regroup_x(0)
-        load_regroup_x(1)
+        load_regroup_x(0, (8, 8, 16))
+        load_regroup_x(1, (16, 8, 8))
         quantise_x(0, 0, D)
-        load_regroup_x(2)
-        load_regroup_x(3)
+        load_regroup_x(2, (16, 16))
+        load_regroup_x(3, (16, 8, 8))
         load_w(0, 0)
         load_w(0, 1)
         NS = 2 * NQ
@@ -284,8 +298,8 @@ def tile_primary_capsule_kernel(tc, X, weight, out):
                     scale_store(rp - 1, 1)
                 if rp >= 0:
                     square_sum(rp, 0, 16)
-        quantise_w(last, 0)
-        quantise_w(last, 1)
+        for h in range(8):
+            quantise_w(last, h, 8)
         multiply(last, 0, 4)
         square_sum(last - 1, 16, 24)
         multiply(last, 4, 8)
@@ -299,10 +313,10 @@ def tile_primary_capsule_kernel(tc, X, weight, out):
         reduce_part(last, 2)
         factor(last - 1, 3)
         sum_so_far(last)
-        scale_store(last - 1, 0)
-        scale_store(last - 1, 1)
         multiply(last, 12, 16)
+        scale_store(last - 1, 0, 16, True)
         norm(last)
+        scale_store(last - 1, 1, 16, True)
         for step in range(4):
             factor(last, step)
         for h in range(4):

@@ -124,15 +124,15 @@ def tile_primary_capsule_kernel(tc, X, weight, out):
                 op=ALU.add,
             )
 
-        def regroup_w_vector(q, cc):
+        def regroup_w_vector(q, cc, i_lo=0, i_hi=IC):
             if cc == 0:
                 st["gw", q] = gwp.tile([P, D, IQ, T], BF16, name="gw", align_bytes=64)
             gw, ws = st["gw", q], st["ws", q, cc]
             wv = WV0 if q == 0 else WV
             if wv > 0:
                 nc.vector.tensor_copy(
-                    out=gw[:, 0:4 * wv, cc * IC:(cc + 1) * IC, :].rearrange("p (g e) i t -> p g i t e", e=4),
-                    in_=ws[:, :, :, 0:4 * wv].rearrange("p i t (g e) -> p g i t e", e=4),
+                    out=gw[:, 0:4 * wv, cc * IC + i_lo:cc * IC + i_hi, :].rearrange("p (g e) i t -> p g i t e", e=4),
+                    in_=ws[:, i_lo:i_hi, :, 0:4 * wv].rearrange("p i t (g e) -> p g i t e", e=4),
                 )
 
         def regroup_w_scalar(q, cc):
@@ -281,18 +281,19 @@ def tile_primary_capsule_kernel(tc, X, weight, out):
             else:
                 if rp >= 0:
                     multiply(rp, 8, 16)
-                if rp >= 1:
-                    factor(rp - 1, 1)
                 add_w(r, cc, 0)
                 if rp >= 1:
-                    factor(rp - 1, 2)
+                    factor(rp - 1, 1)
                 add_w(r, cc, 1)
                 if n == 1:
                     quantise_x(1, D // 2, D)
                 if rp >= 1:
-                    factor(rp - 1, 3)
-                regroup_w_vector(r, cc)
+                    factor(rp - 1, 2)
+                regroup_w_vector(r, cc, 0, IC // 2)
                 regroup_w_scalar(r, cc)
+                if rp >= 1:
+                    factor(rp - 1, 3)
+                regroup_w_vector(r, cc, IC // 2, IC)
                 if rp >= 1:
                     scale_store(rp - 1, 0)
                     scale_store(rp - 1, 1)

@@ -20,21 +20,19 @@ D = 64
 T = 4
 BC = 32
 IC = 16
-IQ = 32
 DK = 16
-NQ = I // IQ
 KIB = 1024
-PIN = True
 XV = 10
 WV = 8
 WV0 = 0
+ROUNDS = (2, 2, 2, 2)
+XP = ((8, 8, 16), (16, 8, 8), (16, 16), (16, 8, 8))
 
 
 def tile_primary_capsule_kernel(tc, X, weight, out):
     nc = tc.nc
     with ExitStack() as ctx:
-        if PIN:
-            ctx.enter_context(tc.manual_schedule())
+        ctx.enter_context(tc.manual_schedule())
         raw = ctx.enter_context(tc.tile_pool(name="raw", bufs=3))
         keep = ctx.enter_context(tc.tile_pool(name="keep", bufs=1))
         gwp = ctx.enter_context(tc.tile_pool(name="gwp", bufs=2))
@@ -59,7 +57,17 @@ def tile_primary_capsule_kernel(tc, X, weight, out):
             gxk = over.tile([P, DK, B, T], BF16, name="gx%d" % k, align_bytes=64, offset=k * 16 * KIB)
             gx.append(gxk)
 
-        def load_regroup_x(c, pieces):
+        st = {}
+        first_load = [sum(ROUNDS[:q]) for q in range(len(ROUNDS))]
+        round_of = {}
+        for q in range(len(ROUNDS)):
+            for c in range(ROUNDS[q]):
+                round_of[first_load[q] + c] = (q, c)
+
+        def iq_of(q):
+            return ROUNDS[q] * IC
+
+        def load_x(c, pieces):
             xr = raw.tile([P, BC, T, D], BF16, tag="raw", name="xr")
             b0 = 0
             for rows in pieces:
@@ -68,15 +76,18 @@ def tile_primary_capsule_kernel(tc, X, weight, out):
                     in_=x_view[:, c * BC + b0:c * BC + b0 + rows, :],
                 )
                 b0 += rows
+            st["xr", c] = xr
+
+        def regroup_x_pieces(c, pieces, xv=XV):
             b0 = 0
             for rows in pieces:
-                regroup_x(xr, c, b0, rows)
+                regroup_x(st["xr", c], c, b0, rows, xv)
                 b0 += rows
 
-        def regroup_x(xr, c, b0, rows):
+        def regroup_x(xr, c, b0, rows, xv):
             for k in range(D // DK):
                 g_lo = k * (DK // 4)
-                nv = max(0, min(DK // 4, XV - g_lo))
+                nv = max(0, min(DK // 4, xv - g_lo))
                 dst = gx[k][:, :, c * BC + b0:c * BC + b0 + rows, :]
                 src = xr[:, b0:b0 + rows, :, k * DK:(k + 1) * DK]
                 if nv > 0:
@@ -99,24 +110,23 @@ def tile_primary_capsule_kernel(tc, X, weight, out):
                     in_=gx[d // DK][:, d % DK, h * 64:(h + 1) * 64, :].rearrange("p b t -> p (b t)"),
                 )
 
-        st = {}
-
-        def load_w(q, cc):
-            i0 = q * IQ + cc * IC
+        def load_w(n, pieces=(8, 8)):
             wr = raw.tile([P, IC * T, 2, D], BF16, tag="raw", name="wr")
-            for h in range(2):
+            lo = 0
+            for n_i in pieces:
                 nc.sync.dma_start(
-                    out=wr[:, h * IC * T // 2:(h + 1) * IC * T // 2, :, :].rearrange("p (i t) k d -> p i (t k d)", t=T),
-                    in_=w_view[:, i0 + h * IC // 2:i0 + (h + 1) * IC // 2, :],
+                    out=wr[:, lo * T:(lo + n_i) * T, :, :].rearrange("p (i t) k d -> p i (t k d)", t=T),
+                    in_=w_view[:, n * IC + lo:n * IC + lo + n_i, :],
                 )
-            st["wr", q, cc] = wr
+                lo += n_i
+            st["wr", n] = wr
 
-        def add_w(q, cc, h):
-            wr = st["wr", q, cc]
-            if h == 0:
-                st["ws", q, cc] = wsp.tile([P, IC, T, D], BF16, name="ws")
-            ws = st["ws", q, cc]
-            rows = slice(h * IC * T // 2, (h + 1) * IC * T // 2)
+        def add_w(n, i_lo, i_hi):
+            wr = st["wr", n]
+            if i_lo == 0:
+                st["ws", n] = wsp.tile([P, IC, T, D], BF16, name="ws")
+            ws = st["ws", n]
+            rows = slice(i_lo * T, i_hi * T)
             nc.vector.tensor_tensor(
                 out=ws[:].rearrange("p i t d -> p (i t) d")[:, rows, :],
                 in0=wr[:, rows, 0, :],
@@ -124,85 +134,100 @@ def tile_primary_capsule_kernel(tc, X, weight, out):
                 op=ALU.add,
             )
 
-        def regroup_w_vector(q, cc, i_lo=0, i_hi=IC):
-            if cc == 0:
-                st["gw", q] = gwp.tile([P, D, IQ, T], BF16, name="gw", align_bytes=64)
-            gw, ws = st["gw", q], st["ws", q, cc]
-            wv = WV0 if q == 0 else WV
+        def gw_of(n):
+            q, c = round_of[n]
+            if ("gw", q) not in st:
+                st["gw", q] = gwp.tile([P, D, iq_of(q), T], BF16, name="gw", align_bytes=64)
+            return st["gw", q], c * IC
+
+        def regroup_v(n, i_lo, i_hi, wv):
+            gw, base = gw_of(n)
+            ws = st["ws", n]
             if wv > 0:
                 nc.vector.tensor_copy(
-                    out=gw[:, 0:4 * wv, cc * IC + i_lo:cc * IC + i_hi, :].rearrange("p (g e) i t -> p g i t e", e=4),
+                    out=gw[:, 0:4 * wv, base + i_lo:base + i_hi, :].rearrange("p (g e) i t -> p g i t e", e=4),
                     in_=ws[:, i_lo:i_hi, :, 0:4 * wv].rearrange("p i t (g e) -> p g i t e", e=4),
                 )
 
-        def regroup_w_scalar(q, cc):
-            gw, ws = st["gw", q], st["ws", q, cc]
-            for g in range(WV0 if q == 0 else WV, D // 4, 4):
+        def regroup_s(n, i_lo, i_hi, wv):
+            gw, base = gw_of(n)
+            ws = st["ws", n]
+            for g in range(wv, D // 4, 4):
                 nc.scalar.copy(
-                    out=gw[:, 4 * g:4 * g + 16, cc * IC:(cc + 1) * IC, :].rearrange("p (g e) i t -> p g i t e", e=4),
-                    in_=ws[:, :, :, 4 * g:4 * g + 16].rearrange("p i t (g e) -> p g i t e", e=4),
+                    out=gw[:, 4 * g:4 * g + 16, base + i_lo:base + i_hi, :].rearrange("p (g e) i t -> p g i t e", e=4),
+                    in_=ws[:, i_lo:i_hi, :, 4 * g:4 * g + 16].rearrange("p i t (g e) -> p g i t e", e=4),
                 )
 
-        def quantise_w(q, h, parts=2):
-            if h == 0:
-                w_codes = wq.tile([P, D * IQ], U32, align_bytes=64, name="w_codes")
-                w_scales = wq.tile([P, D * IQ], U8, align_bytes=64, name="w_scales")
+        S_OFF = (0, 8, 16, 0)
+        Q_OFF = (24, 32, 24, 32)
+
+        def quantise_w(q, h, parts):
+            iq = iq_of(q)
+            if ("codes", q) not in st:
+                w_codes = wq.tile([P, D * iq], U32, align_bytes=64, name="w_codes")
+                w_scales = wq.tile([P, D * iq], U8, align_bytes=64, name="w_scales")
                 st["codes", q] = (w_codes, w_scales)
-                st["s", q] = over.tile([P, IQ, D], F32, name="s_sb%d" % q, offset=(q % 3) * 8 * KIB)
-                st["sq", q] = over.tile([P, IQ, D], F32, name="sq%d" % q, offset=(3 + q % 2) * 8 * KIB)
             w_codes, w_scales = st["codes", q]
             gflat = st["gw", q][:].rearrange("p d i t -> p (d i t)")
-            words = D * IQ // parts
+            words = D * iq // parts
             nc.vector.quantize_mx(
                 out=w_codes[:, h * words:(h + 1) * words].bitcast(FP8X4),
                 scales=w_scales[:, h * words:(h + 1) * words],
                 in_=gflat[:, h * words * T:(h + 1) * words * T],
             )
 
-        def multiply(q, m_lo, m_hi):
+        def multiply(q, m_lo, m_hi, split=False):
+            iq = iq_of(q)
+            nd = 128 // iq
             w_codes, w_scales = st["codes", q]
+            if ("s", q) not in st:
+                st["s", q] = over.tile([P, iq, D], F32, name="s_sb%d" % q, offset=S_OFF[q] * KIB)
+                st["sq", q] = over.tile([P, iq, D], F32, name="sq%d" % q, offset=Q_OFF[q] * KIB)
             s_sb = st["s", q]
             for m in range(m_lo, m_hi):
                 bank = psum.tile([P, 512], F32, name="bank")
                 for r in range(4):
                     d = 4 * m + r
+                    w = d // nd
                     nc.tensor.matmul_mx(
                         out=bank[:, r * 128:(r + 1) * 128],
                         lhsT=x_codes[:, d * B:(d + 1) * B].bitcast(FP8X4),
                         lhsT_scale=x_scales[:, d * B:(d + 1) * B],
-                        rhs=w_codes[:, m * 128:(m + 1) * 128].bitcast(FP8X4),
-                        rhs_scale=w_scales[:, m * 128:(m + 1) * 128],
+                        rhs=w_codes[:, w * 128:(w + 1) * 128].bitcast(FP8X4),
+                        rhs_scale=w_scales[:, w * 128:(w + 1) * 128],
                         start=True,
                         stop=True,
                     )
-                diag = bank[:].rearrange("p (a c) -> p a c", c=IQ)[:, 0:16:5, :]
+                a0 = (4 * m) % nd
+                diag = bank[:].rearrange("p (a c) -> p a c", c=iq)[:, a0:a0 + 3 * (nd + 1) + 1:nd + 1, :]
                 diag = diag.rearrange("p r i -> p i r")
-                if q == NQ - 1:
+                if split:
                     nc.scalar.activation(out=st["sq", q][:, :, 4 * m:4 * m + 4], in_=diag, func=ACT.Square)
                     nc.vector.tensor_copy(out=s_sb[:, :, 4 * m:4 * m + 4], in_=diag)
                 else:
                     nc.scalar.copy(out=s_sb[:, :, 4 * m:4 * m + 4], in_=diag)
 
         def square_sum(q, i_lo, i_hi):
+            iq = iq_of(q)
             if i_lo == 0:
-                st["acc", q] = small.tile([P, IQ], F32, name="n2")
+                st["acc", q] = small.tile([P, iq], F32, name="n2")
             n2 = st["acc", q]
             for i in range(i_lo, i_hi):
                 nc.scalar.activation(
                     out=st["sq", q][:, i, :], in_=st["s", q][:, i, :], func=ACT.Square, accum_out=n2[:, i:i + 1]
                 )
-            if i_hi == IQ:
+            if i_hi == iq:
                 root(q, n2)
 
         def root(q, n2):
-            rt = small.tile([P, IQ], F32, name="rt")
+            rt = small.tile([P, iq_of(q)], F32, name="rt")
             nc.scalar.activation(out=rt[:], in_=n2[:], func=ACT.Sqrt)
             st["n2", q] = (n2, rt)
 
         def reduce_part(q, a):
             sq = st["sq", q]
             if a == 0:
-                st["n2p", q] = small.tile([P, 4, IQ], F32, name="n2p")
+                st["n2p", q] = small.tile([P, 4, iq_of(q)], F32, name="n2p")
             n2p = st["n2p", q]
             nc.vector.tensor_reduce(out=n2p[:, a, :], in_=sq[:, :, 16 * a:16 * a + 16], axis=AX.X, op=ALU.add)
 
@@ -212,113 +237,147 @@ def tile_primary_capsule_kernel(tc, X, weight, out):
             )
 
         def norm(q):
-            n2 = small.tile([P, IQ], F32, name="n2")
+            n2 = small.tile([P, iq_of(q)], F32, name="n2")
             nc.vector.tensor_reduce(out=n2[:], in_=st["sq", q][:, :, 47:D], axis=AX.X, op=ALU.add)
             root(q, n2)
 
         def factor(q, step):
             n2, rt = st["n2", q]
+            iq = iq_of(q)
             if step == 0:
-                st["den", q] = small.tile([P, IQ], F32, name="den")
+                st["den", q] = small.tile([P, iq], F32, name="den")
                 nc.vector.tensor_scalar_add(out=st["den", q][:], in0=n2[:], scalar1=1.0)
             if step == 1:
-                st["den2", q] = small.tile([P, IQ], F32, name="den2")
+                st["den2", q] = small.tile([P, iq], F32, name="den2")
                 nc.vector.scalar_tensor_tensor(
                     out=st["den2", q][:], in0=rt[:], scalar=1e-8, in1=st["den", q][:], op0=ALU.add, op1=ALU.mult
                 )
             if step == 2:
-                st["rec", q] = small.tile([P, IQ], F32, name="rec")
+                st["rec", q] = small.tile([P, iq], F32, name="rec")
                 nc.vector.reciprocal(out=st["rec", q][:], in_=st["den2", q][:])
             if step == 3:
-                st["f", q] = small.tile([P, IQ], F32, name="f")
+                st["f", q] = small.tile([P, iq], F32, name="f")
                 nc.vector.tensor_tensor(out=st["f", q][:], in0=n2[:], in1=st["rec", q][:], op=ALU.mult)
 
-        def scale_store(q, h, n_rows=16, on_scalar=False):
+        def scale_store(q, lo, hi, on_scalar=False, store_now=True):
             s_sb = st["s", q]
-            rows = slice(h * n_rows, (h + 1) * n_rows)
+            rows = slice(lo, hi)
             if on_scalar:
-                for i in range(h * n_rows, (h + 1) * n_rows):
+                for i in range(lo, hi):
                     nc.scalar.activation(out=s_sb[:, i, :], in_=s_sb[:, i, :], func=ACT.Copy, scale=st["f", q][:, i:i + 1])
             else:
                 nc.vector.tensor_tensor(
                     out=s_sb[:, rows, :],
                     in0=s_sb[:, rows, :],
-                    in1=st["f", q][:, rows].unsqueeze(2).to_broadcast([P, n_rows, D]),
+                    in1=st["f", q][:, rows].unsqueeze(2).to_broadcast([P, hi - lo, D]),
                     op=ALU.mult,
                 )
-            nc.sync.dma_start(out=out[:, q * IQ + h * n_rows:q * IQ + (h + 1) * n_rows, :], in_=s_sb[:, rows, :])
+            if store_now:
+                store(q, lo, hi)
 
-        load_regroup_x(0, (8, 8, 16))
-        load_regroup_x(1, (16, 8, 8))
+        def store(q, lo, hi):
+            i0 = first_load[q] * IC
+            nc.sync.dma_start(out=out[:, i0 + lo:i0 + hi, :], in_=st["s", q][:, lo:hi, :])
+
+        load_w(0)
+        load_w(1)
+        load_x(0, XP[0])
+        for n in range(2):
+            add_w(n, 0, 8)
+            add_w(n, 8, 16)
+            regroup_v(n, 0, 16, 0)
+            regroup_s(n, 0, 16, 0)
+            load_x(1 + n, XP[1 + n])
+        regroup_x_pieces(0, XP[0])
+        load_x(3, XP[3])
+        regroup_x_pieces(1, XP[1])
+        load_w(2)
         quantise_x(0, 0, D)
-        load_regroup_x(2, (16, 16))
-        load_regroup_x(3, (16, 8, 8))
-        load_w(0, 0)
-        load_w(0, 1)
-        NS = 2 * NQ
-        last = NQ - 1
-        for n in range(NS):
-            r, cc = n // 2, n % 2
-            rp = r - 1
-            if n + 2 < NS:
-                load_w((n + 2) // 2, n % 2)
-            if cc == 0:
-                add_w(r, cc, 0)
-                add_w(r, cc, 1)
-                if n == 0:
-                    quantise_x(1, 0, D // 2)
-                if rp >= 1:
-                    square_sum(rp - 1, 16, 32)
-                if rp >= 0:
-                    quantise_w(rp, 0)
-                regroup_w_vector(r, cc)
-                regroup_w_scalar(r, cc)
-                if rp >= 0:
-                    quantise_w(rp, 1)
-                    multiply(rp, 0, 8)
-                if rp >= 1:
-                    factor(rp - 1, 0)
-            else:
-                if rp >= 0:
-                    multiply(rp, 8, 16)
-                add_w(r, cc, 0)
-                if rp >= 1:
-                    factor(rp - 1, 1)
-                add_w(r, cc, 1)
-                if n == 1:
-                    quantise_x(1, D // 2, D)
-                if rp >= 1:
-                    factor(rp - 1, 2)
-                regroup_w_vector(r, cc, 0, IC // 2)
-                regroup_w_scalar(r, cc)
-                if rp >= 1:
-                    factor(rp - 1, 3)
-                regroup_w_vector(r, cc, IC // 2, IC)
-                if rp >= 1:
-                    scale_store(rp - 1, 0)
-                    scale_store(rp - 1, 1)
-                if rp >= 0:
-                    square_sum(rp, 0, 16)
+        quantise_w(0, 0, 2)
+        quantise_w(0, 1, 2)
+        regroup_x_pieces(2, XP[2], 6)
+        load_w(3)
+        regroup_x_pieces(3, XP[3], 6)
+        quantise_x(1, 0, D // 2)
+        multiply(0, 0, 8)
+        quantise_x(1, D // 2, D)
+        multiply(0, 8, 16)
+        load_w(4)
+        add_w(2, 0, 8)
+        add_w(2, 8, 16)
+        regroup_v(2, 0, 16, 8)
+        regroup_s(2, 0, 16, 8)
+        load_w(5)
+        add_w(3, 0, 8)
+        add_w(3, 8, 16)
+        regroup_v(3, 0, 8, 8)
+        regroup_s(3, 0, 16, 8)
+        regroup_v(3, 8, 16, 8)
+        square_sum(0, 0, 16)
+        load_w(6)
+        add_w(4, 0, 8)
+        add_w(4, 8, 16)
+        square_sum(0, 16, 32)
+        quantise_w(1, 0, 2)
+        regroup_v(4, 0, 16, 8)
+        regroup_s(4, 0, 16, 8)
+        quantise_w(1, 1, 2)
+        multiply(1, 0, 8)
+        factor(0, 0)
+        load_w(7, (8, 8))
+        multiply(1, 8, 16)
+        add_w(5, 0, 8)
+        factor(0, 1)
+        add_w(5, 8, 16)
+        factor(0, 2)
+        regroup_v(5, 0, 8, 8)
+        regroup_s(5, 0, 16, 8)
+        factor(0, 3)
+        regroup_v(5, 8, 16, 8)
+        scale_store(0, 0, 16)
+        scale_store(0, 16, 32)
+        square_sum(1, 0, 16)
+        add_w(6, 0, 8)
+        add_w(6, 8, 16)
+        square_sum(1, 16, 32)
+        quantise_w(2, 0, 2)
+        regroup_v(6, 0, 16, 8)
+        regroup_s(6, 0, 16, 8)
+        quantise_w(2, 1, 2)
+        multiply(2, 0, 8)
+        factor(1, 0)
+        multiply(2, 8, 16)
+        add_w(7, 0, 8)
+        factor(1, 1)
+        add_w(7, 8, 16)
+        factor(1, 2)
+        regroup_v(7, 0, 8, 8)
+        regroup_s(7, 0, 16, 8)
+        factor(1, 3)
+        regroup_v(7, 8, 16, 8)
+        scale_store(1, 0, 16)
+        scale_store(1, 16, 32)
+        square_sum(2, 0, 16)
         for h in range(8):
-            quantise_w(last, h, 8)
-        multiply(last, 0, 4)
-        square_sum(last - 1, 16, 24)
-        multiply(last, 4, 8)
-        square_sum(last - 1, 24, 32)
-        reduce_part(last, 0)
-        factor(last - 1, 0)
-        factor(last - 1, 1)
-        multiply(last, 8, 12)
-        reduce_part(last, 1)
-        factor(last - 1, 2)
-        reduce_part(last, 2)
-        factor(last - 1, 3)
-        sum_so_far(last)
-        multiply(last, 12, 16)
-        scale_store(last - 1, 0, 16, True)
-        norm(last)
-        scale_store(last - 1, 1, 16, True)
+            quantise_w(3, h, 8)
+        multiply(3, 0, 4, True)
+        square_sum(2, 16, 24)
+        multiply(3, 4, 8, True)
+        square_sum(2, 24, 32)
+        reduce_part(3, 0)
+        factor(2, 0)
+        factor(2, 1)
+        multiply(3, 8, 12, True)
+        reduce_part(3, 1)
+        factor(2, 2)
+        reduce_part(3, 2)
+        factor(2, 3)
+        sum_so_far(3)
+        multiply(3, 12, 16, True)
+        scale_store(2, 0, 16, True)
+        norm(3)
+        scale_store(2, 16, 32, True)
         for step in range(4):
-            factor(last, step)
+            factor(3, step)
         for h in range(4):
-            scale_store(last, h, 8)
+            scale_store(3, 8 * h, 8 * h + 8)

@@ -303,6 +303,7 @@ def tile_primary_capsule_kernel(tc, X, weight, out):
         quantise_x(1, D // 2, D)
         multiply(0, 8, 16)
         load_w(4)
+        square_sum(0, 0, 32)
         add_w(2, 0, 8)
         add_w(2, 8, 16)
         regroup_v(2, 0, 16, 8)
@@ -310,41 +311,41 @@ def tile_primary_capsule_kernel(tc, X, weight, out):
         load_w(5)
         add_w(3, 0, 8)
         add_w(3, 8, 16)
+        factor(0, 0)
         regroup_v(3, 0, 8, 8)
         regroup_s(3, 0, 16, 8)
+        factor(0, 1)
         regroup_v(3, 8, 16, 8)
-        square_sum(0, 0, 16)
+        factor(0, 2)
         load_w(6)
-        add_w(4, 0, 8)
-        add_w(4, 8, 16)
-        square_sum(0, 16, 32)
         quantise_w(1, 0, 2)
+        multiply(1, 0, 8)
+        add_w(4, 0, 8)
+        factor(0, 3)
+        scale_store(0, 0, 16, False, False)
+        add_w(4, 8, 16)
+        quantise_w(1, 1, 2)
         regroup_v(4, 0, 16, 8)
         regroup_s(4, 0, 16, 8)
-        quantise_w(1, 1, 2)
-        multiply(1, 0, 8)
-        factor(0, 0)
-        load_w(7, (8, 8))
         multiply(1, 8, 16)
+        scale_store(0, 16, 32, False, False)
+        load_w(7, (8, 8))
+        store(0, 0, 16)
+        store(0, 16, 32)
+        square_sum(1, 0, 16)
         add_w(5, 0, 8)
-        factor(0, 1)
         add_w(5, 8, 16)
-        factor(0, 2)
         regroup_v(5, 0, 8, 8)
         regroup_s(5, 0, 16, 8)
-        factor(0, 3)
         regroup_v(5, 8, 16, 8)
-        scale_store(0, 0, 16)
-        scale_store(0, 16, 32)
-        square_sum(1, 0, 16)
-        add_w(6, 0, 8)
-        add_w(6, 8, 16)
         square_sum(1, 16, 32)
         quantise_w(2, 0, 2)
+        multiply(2, 0, 8)
+        add_w(6, 0, 8)
+        add_w(6, 8, 16)
+        quantise_w(2, 1, 2)
         regroup_v(6, 0, 16, 8)
         regroup_s(6, 0, 16, 8)
-        quantise_w(2, 1, 2)
-        multiply(2, 0, 8)
         factor(1, 0)
         multiply(2, 8, 16)
         add_w(7, 0, 8)
@@ -355,23 +356,25 @@ def tile_primary_capsule_kernel(tc, X, weight, out):
         regroup_s(7, 0, 16, 8)
         factor(1, 3)
         regroup_v(7, 8, 16, 8)
-        scale_store(1, 0, 16)
-        scale_store(1, 16, 32)
         square_sum(2, 0, 16)
         for h in range(8):
             quantise_w(3, h, 8)
+        scale_store(1, 0, 8)
         multiply(3, 0, 4, True)
         square_sum(2, 16, 24)
+        scale_store(1, 8, 16)
         multiply(3, 4, 8, True)
         square_sum(2, 24, 32)
         reduce_part(3, 0)
+        scale_store(1, 16, 24)
         factor(2, 0)
-        factor(2, 1)
         multiply(3, 8, 12, True)
+        factor(2, 1)
         reduce_part(3, 1)
         factor(2, 2)
-        reduce_part(3, 2)
+        scale_store(1, 24, 32)
         factor(2, 3)
+        reduce_part(3, 2)
         sum_so_far(3)
         multiply(3, 12, 16, True)
         scale_store(2, 0, 16, True)

@@ -32,7 +32,6 @@ XP = ((8, 8, 16), (16, 8, 8), (16, 16), (16, 8, 8))
 def tile_primary_capsule_kernel(tc, X, weight, out):
     nc = tc.nc
     with ExitStack() as ctx:
-        ctx.enter_context(tc.manual_schedule())
         raw = ctx.enter_context(tc.tile_pool(name="raw", bufs=3))
         keep = ctx.enter_context(tc.tile_pool(name="keep", bufs=1))
         gwp = ctx.enter_context(tc.tile_pool(name="gwp", bufs=2))

@@ -365,21 +365,23 @@ def tile_primary_capsule_kernel(tc, X, weight, out):
         multiply(3, 4, 8, True)
         square_sum(2, 24, 32)
         reduce_part(3, 0)
-        scale_store(1, 16, 24)
         factor(2, 0)
         multiply(3, 8, 12, True)
         factor(2, 1)
         reduce_part(3, 1)
         factor(2, 2)
-        scale_store(1, 24, 32)
         factor(2, 3)
         reduce_part(3, 2)
         sum_so_far(3)
         multiply(3, 12, 16, True)
+        scale_store(1, 16, 32, True)
         scale_store(2, 0, 16, True)
         norm(3)
         scale_store(2, 16, 32, True)
         for step in range(4):
             factor(3, step)
-        for h in range(4):
-            scale_store(3, 8 * h, 8 * h + 8)
+        scale_store(3, 0, 8)
+        scale_store(3, 20, 26, True)
+        scale_store(3, 8, 16)
+        scale_store(3, 26, 32, True)
+        scale_store(3, 16, 20)

from contextlib import ExitStack

import concourse.mybir as mybir

FLOPS = 2 * 128 * 128 * 512 * 64

BF16 = mybir.dt.bfloat16
F32 = mybir.dt.float32
U32 = mybir.dt.uint32
U8 = mybir.dt.uint8
FP8X4 = mybir.dt.float8_e4m3fn_x4
ACT = mybir.ActivationFunctionType
ALU = mybir.AluOpType
AX = mybir.AxisListType

P = 128
B = 128
I = 128
D = 64
T = 4
BC = 32
IC = 16
DK = 16
KIB = 1024
XV = 10
WV = 8
WV0 = 0
ROUNDS = (2, 2, 2, 2)
XP = ((8, 8, 16), (16, 8, 8), (16, 16), (16, 8, 8))


def tile_primary_capsule_kernel(tc, X, weight, out):
    nc = tc.nc
    with ExitStack() as ctx:
        raw = ctx.enter_context(tc.tile_pool(name="raw", bufs=3))
        keep = ctx.enter_context(tc.tile_pool(name="keep", bufs=1))
        gwp = ctx.enter_context(tc.tile_pool(name="gwp", bufs=2))
        wq = ctx.enter_context(tc.tile_pool(name="wq", bufs=2))
        wsp = ctx.enter_context(tc.tile_pool(name="wsp", bufs=2))
        small = ctx.enter_context(tc.tile_pool(name="small", bufs=2))
        over = ctx.enter_context(tc.tile_pool(name="over", bufs=1))
        psum = ctx.enter_context(tc.psum_pool(name="psum", bufs=8))

        warm = keep.tile([P, 1], F32)
        nc.vector.memset(warm[:], 1.0)
        nc.scalar.activation(out=warm[:], in_=warm[:], func=ACT.Sqrt)

        x_view = X.rearrange("b (p t) d -> p b (t d)", t=T)
        w_view = weight.rearrange("i (p t) k d -> p i (t k d)", t=T)

        x_codes = keep.tile([P, D * B], U32, align_bytes=64)
        x_scales = keep.tile([P, D * B], U8, align_bytes=64)

        gx = []
        for k in range(D // DK):
            gxk = over.tile([P, DK, B, T], BF16, name="gx%d" % k, align_bytes=64, offset=k * 16 * KIB)
            gx.append(gxk)

        st = {}
        first_load = [sum(ROUNDS[:q]) for q in range(len(ROUNDS))]
        round_of = {}
        for q in range(len(ROUNDS)):
            for c in range(ROUNDS[q]):
                round_of[first_load[q] + c] = (q, c)

        def iq_of(q):
            return ROUNDS[q] * IC

        def load_x(c, pieces):
            xr = raw.tile([P, BC, T, D], BF16, tag="raw", name="xr")
            b0 = 0
            for rows in pieces:
                nc.sync.dma_start(
                    out=xr[:, b0:b0 + rows, :, :].rearrange("p b t d -> p b (t d)"),
                    in_=x_view[:, c * BC + b0:c * BC + b0 + rows, :],
                )
                b0 += rows
            st["xr", c] = xr

        def regroup_x_pieces(c, pieces, xv=XV):
            b0 = 0
            for rows in pieces:
                regroup_x(st["xr", c], c, b0, rows, xv)
                b0 += rows

        def regroup_x(xr, c, b0, rows, xv):
            for k in range(D // DK):
                g_lo = k * (DK // 4)
                nv = max(0, min(DK // 4, xv - g_lo))
                dst = gx[k][:, :, c * BC + b0:c * BC + b0 + rows, :]
                src = xr[:, b0:b0 + rows, :, k * DK:(k + 1) * DK]
                if nv > 0:
                    nc.vector.tensor_copy(
                        out=dst[:, 0:4 * nv, :, :].rearrange("p (g e) b t -> p g b t e", e=4),
                        in_=src[:, :, :, 0:4 * nv].rearrange("p b t (g e) -> p g b t e", e=4),
                    )
                if nv < DK // 4:
                    nc.scalar.copy(
                        out=dst[:, 4 * nv:DK, :, :].rearrange("p (g e) b t -> p g b t e", e=4),
                        in_=src[:, :, :, 4 * nv:DK].rearrange("p b t (g e) -> p g b t e", e=4),
                    )

        def quantise_x(h, d_lo, d_hi):
            for d in range(d_lo, d_hi):
                w0 = d * B + h * 64
                nc.vector.quantize_mx(
                    out=x_codes[:, w0:w0 + 64].bitcast(FP8X4),
                    scales=x_scales[:, w0:w0 + 64],
                    in_=gx[d // DK][:, d % DK, h * 64:(h + 1) * 64, :].rearrange("p b t -> p (b t)"),
                )

        def load_w(n, pieces=(8, 8)):
            wr = raw.tile([P, IC * T, 2, D], BF16, tag="raw", name="wr")
            lo = 0
            for n_i in pieces:
                nc.sync.dma_start(
                    out=wr[:, lo * T:(lo + n_i) * T, :, :].rearrange("p (i t) k d -> p i (t k d)", t=T),
                    in_=w_view[:, n * IC + lo:n * IC + lo + n_i, :],
                )
                lo += n_i
            st["wr", n] = wr

        def add_w(n, i_lo, i_hi):
            wr = st["wr", n]
            if i_lo == 0:
                st["ws", n] = wsp.tile([P, IC, T, D], BF16, name="ws")
            ws = st["ws", n]
            rows = slice(i_lo * T, i_hi * T)
            nc.vector.tensor_tensor(
                out=ws[:].rearrange("p i t d -> p (i t) d")[:, rows, :],
                in0=wr[:, rows, 0, :],
                in1=wr[:, rows, 1, :],
                op=ALU.add,
            )

        def gw_of(n):
            q, c = round_of[n]
            if ("gw", q) not in st:
                st["gw", q] = gwp.tile([P, D, iq_of(q), T], BF16, name="gw", align_bytes=64)
            return st["gw", q], c * IC

        def regroup_v(n, i_lo, i_hi, wv):
            gw, base = gw_of(n)
            ws = st["ws", n]
            if wv > 0:
                nc.vector.tensor_copy(
                    out=gw[:, 0:4 * wv, base + i_lo:base + i_hi, :].rearrange("p (g e) i t -> p g i t e", e=4),
                    in_=ws[:, i_lo:i_hi, :, 0:4 * wv].rearrange("p i t (g e) -> p g i t e", e=4),
                )

        def regroup_s(n, i_lo, i_hi, wv):
            gw, base = gw_of(n)
            ws = st["ws", n]
            for g in range(wv, D // 4, 4):
                nc.scalar.copy(
                    out=gw[:, 4 * g:4 * g + 16, base + i_lo:base + i_hi, :].rearrange("p (g e) i t -> p g i t e", e=4),
                    in_=ws[:, i_lo:i_hi, :, 4 * g:4 * g + 16].rearrange("p i t (g e) -> p g i t e", e=4),
                )

        S_OFF = (0, 8, 16, 0)
        Q_OFF = (24, 32, 24, 32)

        def quantise_w(q, h, parts):
            iq = iq_of(q)
            if ("codes", q) not in st:
                w_codes = wq.tile([P, D * iq], U32, align_bytes=64, name="w_codes")
                w_scales = wq.tile([P, D * iq], U8, align_bytes=64, name="w_scales")
                st["codes", q] = (w_codes, w_scales)
            w_codes, w_scales = st["codes", q]
            gflat = st["gw", q][:].rearrange("p d i t -> p (d i t)")
            words = D * iq // parts
            nc.vector.quantize_mx(
                out=w_codes[:, h * words:(h + 1) * words].bitcast(FP8X4),
                scales=w_scales[:, h * words:(h + 1) * words],
                in_=gflat[:, h * words * T:(h + 1) * words * T],
            )

        def multiply(q, m_lo, m_hi, split=False):
            iq = iq_of(q)
            nd = 128 // iq
            w_codes, w_scales = st["codes", q]
            if ("s", q) not in st:
                st["s", q] = over.tile([P, iq, D], F32, name="s_sb%d" % q, offset=S_OFF[q] * KIB)
                st["sq", q] = over.tile([P, iq, D], F32, name="sq%d" % q, offset=Q_OFF[q] * KIB)
            s_sb = st["s", q]
            for m in range(m_lo, m_hi):
                bank = psum.tile([P, 512], F32, name="bank")
                for r in range(4):
                    d = 4 * m + r
                    w = d // nd
                    nc.tensor.matmul_mx(
                        out=bank[:, r * 128:(r + 1) * 128],
                        lhsT=x_codes[:, d * B:(d + 1) * B].bitcast(FP8X4),
                        lhsT_scale=x_scales[:, d * B:(d + 1) * B],
                        rhs=w_codes[:, w * 128:(w + 1) * 128].bitcast(FP8X4),
                        rhs_scale=w_scales[:, w * 128:(w + 1) * 128],
                        start=True,
                        stop=True,
                    )
                a0 = (4 * m) % nd
                diag = bank[:].rearrange("p (a c) -> p a c", c=iq)[:, a0:a0 + 3 * (nd + 1) + 1:nd + 1, :]
                diag = diag.rearrange("p r i -> p i r")
                if split:
                    nc.scalar.activation(out=st["sq", q][:, :, 4 * m:4 * m + 4], in_=diag, func=ACT.Square)
                    nc.vector.tensor_copy(out=s_sb[:, :, 4 * m:4 * m + 4], in_=diag)
                else:
                    nc.scalar.copy(out=s_sb[:, :, 4 * m:4 * m + 4], in_=diag)

        def square_sum(q, i_lo, i_hi):
            iq = iq_of(q)
            if i_lo == 0:
                st["acc", q] = small.tile([P, iq], F32, name="n2")
            n2 = st["acc", q]
            for i in range(i_lo, i_hi):
                nc.scalar.activation(
                    out=st["sq", q][:, i, :], in_=st["s", q][:, i, :], func=ACT.Square, accum_out=n2[:, i:i + 1]
                )
            if i_hi == iq:
                root(q, n2)

        def root(q, n2):
            rt = small.tile([P, iq_of(q)], F32, name="rt")
            nc.scalar.activation(out=rt[:], in_=n2[:], func=ACT.Sqrt)
            st["n2", q] = (n2, rt)

        def reduce_part(q, a):
            sq = st["sq", q]
            if a == 0:
                st["n2p", q] = small.tile([P, 4, iq_of(q)], F32, name="n2p")
            n2p = st["n2p", q]
            nc.vector.tensor_reduce(out=n2p[:, a, :], in_=sq[:, :, 16 * a:16 * a + 16], axis=AX.X, op=ALU.add)

        def sum_so_far(q):
            nc.vector.tensor_reduce(
                out=st["sq", q][:, :, 47], in_=st["n2p", q][:, 0:3, :].rearrange("p a i -> p i a"), axis=AX.X, op=ALU.add
            )

        def norm(q):
            n2 = small.tile([P, iq_of(q)], F32, name="n2")
            nc.vector.tensor_reduce(out=n2[:], in_=st["sq", q][:, :, 47:D], axis=AX.X, op=ALU.add)
            root(q, n2)

        def factor(q, step):
            n2, rt = st["n2", q]
            iq = iq_of(q)
            if step == 0:
                st["den", q] = small.tile([P, iq], F32, name="den")
                nc.vector.tensor_scalar_add(out=st["den", q][:], in0=n2[:], scalar1=1.0)
            if step == 1:
                st["den2", q] = small.tile([P, iq], F32, name="den2")
                nc.vector.scalar_tensor_tensor(
                    out=st["den2", q][:], in0=rt[:], scalar=1e-8, in1=st["den", q][:], op0=ALU.add, op1=ALU.mult
                )
            if step == 2:
                st["rec", q] = small.tile([P, iq], F32, name="rec")
                nc.vector.reciprocal(out=st["rec", q][:], in_=st["den2", q][:])
            if step == 3:
                st["f", q] = small.tile([P, iq], F32, name="f")
                nc.vector.tensor_tensor(out=st["f", q][:], in0=n2[:], in1=st["rec", q][:], op=ALU.mult)

        def scale_store(q, lo, hi, on_scalar=False, store_now=True):
            s_sb = st["s", q]
            rows = slice(lo, hi)
            if on_scalar:
                for i in range(lo, hi):
                    nc.scalar.activation(out=s_sb[:, i, :], in_=s_sb[:, i, :], func=ACT.Copy, scale=st["f", q][:, i:i + 1])
            else:
                nc.vector.tensor_tensor(
                    out=s_sb[:, rows, :],
                    in0=s_sb[:, rows, :],
                    in1=st["f", q][:, rows].unsqueeze(2).to_broadcast([P, hi - lo, D]),
                    op=ALU.mult,
                )
            if store_now:
                store(q, lo, hi)

        def store(q, lo, hi):
            i0 = first_load[q] * IC
            nc.sync.dma_start(out=out[:, i0 + lo:i0 + hi, :], in_=st["s", q][:, lo:hi, :])

        load_w(0)
        load_w(1)
        load_x(0, XP[0])
        for n in range(2):
            add_w(n, 0, 8)
            add_w(n, 8, 16)
            regroup_v(n, 0, 16, 0)
            regroup_s(n, 0, 16, 0)
            load_x(1 + n, XP[1 + n])
        regroup_x_pieces(0, XP[0])
        load_x(3, XP[3])
        regroup_x_pieces(1, XP[1])
        load_w(2)
        quantise_x(0, 0, D)
        quantise_w(0, 0, 2)
        quantise_w(0, 1, 2)
        regroup_x_pieces(2, XP[2], 6)
        load_w(3)
        regroup_x_pieces(3, XP[3], 6)
        quantise_x(1, 0, D // 2)
        multiply(0, 0, 8)
        quantise_x(1, D // 2, D)
        multiply(0, 8, 16)
        load_w(4)
        square_sum(0, 0, 32)
        add_w(2, 0, 8)
        add_w(2, 8, 16)
        regroup_v(2, 0, 16, 8)
        regroup_s(2, 0, 16, 8)
        load_w(5)
        add_w(3, 0, 8)
        add_w(3, 8, 16)
        factor(0, 0)
        regroup_v(3, 0, 8, 8)
        regroup_s(3, 0, 16, 8)
        factor(0, 1)
        regroup_v(3, 8, 16, 8)
        factor(0, 2)
        load_w(6)
        quantise_w(1, 0, 2)
        multiply(1, 0, 8)
        add_w(4, 0, 8)
        factor(0, 3)
        scale_store(0, 0, 16, False, False)
        add_w(4, 8, 16)
        quantise_w(1, 1, 2)
        regroup_v(4, 0, 16, 8)
        regroup_s(4, 0, 16, 8)
        multiply(1, 8, 16)
        scale_store(0, 16, 32, False, False)
        load_w(7, (8, 8))
        store(0, 0, 16)
        store(0, 16, 32)
        square_sum(1, 0, 16)
        add_w(5, 0, 8)
        add_w(5, 8, 16)
        regroup_v(5, 0, 8, 8)
        regroup_s(5, 0, 16, 8)
        regroup_v(5, 8, 16, 8)
        square_sum(1, 16, 32)
        quantise_w(2, 0, 2)
        multiply(2, 0, 8)
        add_w(6, 0, 8)
        add_w(6, 8, 16)
        quantise_w(2, 1, 2)
        regroup_v(6, 0, 16, 8)
        regroup_s(6, 0, 16, 8)
        factor(1, 0)
        multiply(2, 8, 16)
        add_w(7, 0, 8)
        factor(1, 1)
        add_w(7, 8, 16)
        factor(1, 2)
        regroup_v(7, 0, 8, 8)
        regroup_s(7, 0, 16, 8)
        factor(1, 3)
        regroup_v(7, 8, 16, 8)
        square_sum(2, 0, 16)
        for h in range(8):
            quantise_w(3, h, 8)
        scale_store(1, 0, 8)
        multiply(3, 0, 4, True)
        square_sum(2, 16, 24)
        scale_store(1, 8, 16)
        multiply(3, 4, 8, True)
        square_sum(2, 24, 32)
        reduce_part(3, 0)
        factor(2, 0)
        multiply(3, 8, 12, True)
        factor(2, 1)
        reduce_part(3, 1)
        factor(2, 2)
        factor(2, 3)
        reduce_part(3, 2)
        sum_so_far(3)
        multiply(3, 12, 16, True)
        scale_store(1, 16, 32, True)
        scale_store(2, 0, 16, True)
        norm(3)
        scale_store(2, 16, 32, True)
        for step in range(4):
            factor(3, step)
        scale_store(3, 0, 8)
        scale_store(3, 20, 26, True)
        scale_store(3, 8, 16)
        scale_store(3, 26, 32, True)
        scale_store(3, 16, 20)
